import numpy as np
import ml_dtypes


def mxq(x, axis, fmt="e4m3"):
    dtype, down = {"e4m3": (ml_dtypes.float8_e4m3fn, 7), "e5m2": (ml_dtypes.float8_e5m2, 14)}[fmt]
    v = np.moveaxis(np.asarray(x, np.float32).astype(ml_dtypes.bfloat16).astype(np.float64), axis, -1)
    blocks = v.reshape(v.shape[:-1] + (-1, 32))
    amax = np.abs(blocks).max(-1, keepdims=True)
    byte = np.maximum(np.where(amax > 0, np.frexp(amax)[1] - 1 + 127, 0) - down, 1)
    scale = np.exp2(byte - 127.0)
    codes = (blocks / scale).astype(np.float32).astype(dtype).astype(np.float64)
    return np.moveaxis((codes * scale).reshape(v.shape), -1, axis)


WIDE = False


def mx_kscale(k):
    if not WIDE:
        return np.ones(k)
    levels = np.array([10, -10, 5, -5, 0])
    a = np.random.permutation(np.resize(levels, k // 512 * 4)).reshape(k // 512, 4)
    idx = np.arange(k)
    return np.exp2(a[idx // 512, idx % 128 // 32])


BF16 = ml_dtypes.bfloat16


def bf(x):
    return np.asarray(x, np.float32).astype(BF16)


def f64(x):
    return np.asarray(x).astype(np.float64)


E2M1 = np.array([0.0, 0.5, 1.0, 1.5, 2.0, 3.0, 4.0, 6.0, -0.0, -0.5, -1.0, -1.5, -2.0, -3.0, -4.0, -6.0])


def pack_weight(w, fmt):
    k, n = w.shape
    w = f64(bf(w)).reshape(k // 32, 32, n)
    amax = np.abs(w).max(1)
    if fmt == "e4m3":
        byte = np.frexp(amax)[1] - 1 + 127 - 7
    else:
        mant, ex = np.frexp(amax / 6.0)
        byte = np.where(mant > 0.5, ex, ex - 1) + 127
    byte = np.clip(np.where(amax > 0, byte, 1), 1, 254)
    scaled = (w * np.exp2(127.0 - byte)[:, None, :]).reshape(k, n).astype(np.float32)
    by_word = np.ascontiguousarray(scaled.reshape(k // 512, 128, 4, n).transpose(0, 1, 3, 2))
    if fmt == "e4m3":
        words = by_word.astype(ml_dtypes.float8_e4m3fn).view(np.uint8)
    else:
        c = by_word.astype(ml_dtypes.float4_e2m1fn).view(np.uint8) & 0xF
        words = c[..., 0::2] | (c[..., 1::2] << 4)
    return np.ascontiguousarray(words), np.ascontiguousarray(byte.astype(np.uint8).reshape(k // 512, 16, n))


def unpack_weight(words, scales, fmt):
    g, p, n, _ = words.shape
    if fmt == "e4m3":
        vals = np.ascontiguousarray(words).view(ml_dtypes.float8_e4m3fn).astype(np.float64)
    else:
        nib = np.empty((g, p, n, 4), np.uint8)
        nib[..., 0::2] = words & 0xF
        nib[..., 1::2] = words >> 4
        vals = E2M1[nib]
    vals = vals * np.repeat(np.exp2(scales.astype(np.float64) - 127.0), 8, axis=1)[..., None]
    return vals.transpose(0, 1, 3, 2).reshape(g * 512, n)


B, H, W, FI, FO = 4, 32, 32, 512, 1024

OFFSETS = [(-1, 0), (1, 0), (0, -1), (0, 1), (-1, -1), (-1, 1), (1, -1), (1, 1)]


def setup_inputs():
    s = mx_kscale(FI)
    X = bf(np.random.standard_normal((B, H * W, FI)) * 0.5 * s)
    Wm_words, Wm_scales = pack_weight(np.random.standard_normal((FI, FO)) / np.sqrt(FI) / s[:, None], "e4m3")
    b = bf(np.random.standard_normal(FO) * 0.2)
    return {"X": X,
            "Wm_words": Wm_words,
            "Wm_scales": Wm_scales,
            "b": b,
            "H": H, "W": W}


def reference(X, Wm_words, Wm_scales, b, H, W):
    X = f64(X)
    Bn, N, F = X.shape
    Xg = X.reshape(Bn, H, W, F)
    P = np.pad(Xg, ((0, 0), (1, 1), (1, 1), (0, 0)))
    AX = P[:, 1 + OFFSETS[0][0]:1 + OFFSETS[0][0] + H,
           1 + OFFSETS[0][1]:1 + OFFSETS[0][1] + W, :]
    for dr, dc in OFFSETS[1:]:
        AX = AX + P[:, 1 + dr:1 + dr + H, 1 + dc:1 + dc + W, :]
    AX = AX.reshape(Bn, N, F)
    return (mxq(AX, 2, "e4m3") @ unpack_weight(Wm_words, Wm_scales, "e4m3")) + f64(b)

@@ -1,0 +1,226 @@
+from contextlib import ExitStack
+
+import concourse.mybir as mybir
+from concourse.masks import make_identity
+
+F32 = mybir.dt.float32
+BF16 = mybir.dt.bfloat16
+I32 = mybir.dt.int32
+U32 = mybir.dt.uint32
+U8 = mybir.dt.uint8
+FP8X4 = mybir.dt.float8_e4m3fn_x4
+ADD = mybir.AluOpType.add
+
+P = 128
+PACK = 4
+BANK = 512
+BLOCKS_PER_QUANTISE = 2
+
+FLOPS = 2 * 4 * 1024 * 512 * 1024
+
+
+def tile_graphconvlayer_kernel(tc, X, Wm_words, Wm_scales, b, H, W, out):
+    nc = tc.nc
+    images, nodes, features = X.shape
+    outputs = b.shape[0]
+    assert features == P * PACK, "one matmul_mx pass contracts all features"
+    assert nodes == H * W and P == 4 * W, "a block of 128 nodes is 4 rows of the grid"
+    block_rows = P // W
+    blocks_per_image = nodes // P
+    windows_per_image = 2 * blocks_per_image
+    window_nodes_out = 2 * W
+    last_image = images - 1
+    blocks = images * blocks_per_image
+    word_cols = P * PACK
+    out_rows = out.flatten_outer_dims()
+
+    with ExitStack() as ctx:
+        keep = ctx.enter_context(tc.tile_pool(name="keep", bufs=1))
+        scratch = ctx.enter_context(tc.tile_pool(name="scratch", bufs=2))
+        results = ctx.enter_context(tc.tile_pool(name="results", bufs=6))
+        psum_words = ctx.enter_context(tc.psum_pool(name="psum_words", bufs=2))
+        psum_sums = ctx.enter_context(tc.psum_pool(name="psum_sums", bufs=2))
+        psum_out = ctx.enter_context(tc.psum_pool(name="psum_out", bufs=4))
+
+        ctx.enter_context(tc.manual_schedule())
+
+        w_scales = keep.tile([P, outputs], U8, align_bytes=64)
+        nc.vector.memset(w_scales[:].bitcast(I32), 0)
+        framed = keep.tile([P, H + 2, (W + 2) * PACK], BF16)
+        nc.vector.memset(framed[:].bitcast(F32), 0.0)
+        row_cols = W * PACK
+        threes = keep.tile([P, H + 2, row_cols], F32)
+        nc.vector.memset(threes[:, 0, :], 0.0)
+        nc.vector.memset(threes[:, H + 1, :], 0.0)
+
+        last_nodes = keep.tile([P, blocks_per_image, features], BF16)
+        nc.sync.dma_start(out=last_nodes[:], in_=X[last_image].rearrange("(k p) f -> p k f", p=P))
+        bias_bf16 = keep.tile([P, outputs], BF16)
+        nc.scalar.dma_start(out=bias_bf16[:], in_=b.partition_broadcast(P))
+        for quadrant in range(4):
+            nc.sync.dma_start(
+                out=w_scales[32 * quadrant : 32 * quadrant + 4, :].bitcast(I32),
+                in_=Wm_scales[0, 4 * quadrant : 4 * quadrant + 4, :].bitcast(I32),
+            )
+
+        def window_start(i):
+            return min(max(2 * i - 1, 0), H - block_rows)
+
+        def load_windows(image):
+            windows = keep.tile([P, windows_per_image, features], BF16, name="windows%d" % image)
+            rows = X[image]
+            inner = blocks_per_image - 1
+            nc.sync.dma_start(out=windows[:, 0, :], in_=rows[0:P, :])
+            for first in (1, 2):
+                start = window_start(first) * W
+                nc.sync.dma_start(
+                    out=windows[:, first : first + 2 * inner : 2, :],
+                    in_=rows[start : start + inner * P, :].rearrange("(k p) f -> p k f", p=P),
+                )
+            nc.sync.dma_start(out=windows[:, windows_per_image - 1, :], in_=rows[nodes - P : nodes, :])
+            return windows
+
+        windows_of = [load_windows(0)]
+        w_words = keep.tile([P, outputs], U32, align_bytes=64)
+        nc.sync.dma_start(
+            out=w_words[:].bitcast(I32), in_=Wm_words[0].rearrange("p n t -> p (n t)").bitcast(I32)
+        )
+        for image in range(1, last_image):
+            windows_of.append(load_windows(image))
+
+        identity = keep.tile([P, P], F32)
+        make_identity(nc, identity[:])
+
+        by_column = keep.tile([P, W, 3, 2], BF16)
+        nc.gpsimd.memset(by_column[:], 0.0)
+        for dr in (-1, 0, 1):
+            for dc in (-1, 0, 1):
+                if (dr, dc) != (0, 0):
+                    first = max(0, -dc)
+                    count = W - abs(dc)
+                    diagonal = by_column[:, first : first + count, :, :]
+                    nc.gpsimd.affine_select(
+                        out=diagonal,
+                        in_=diagonal,
+                        compare_op=mybir.AluOpType.not_equal,
+                        fill=1.0,
+                        base=-(W * dr + dc + first),
+                        channel_multiplier=1,
+                        pattern=[[-1, count], [-W, 3], [-W, 2]],
+                    )
+        adjacency = keep.tile([P, 3, 2, W], BF16)
+        nc.vector.tensor_copy(out=adjacency[:], in_=by_column[:].rearrange("p c a r -> p a r c"))
+
+        grouped = keep.tile([P, blocks * word_cols], BF16, align_bytes=64)
+        codes = keep.tile([P, blocks * P], U32, align_bytes=64)
+        scales = keep.tile([P, blocks * P], U8, align_bytes=64)
+
+        framed_words = framed[:].bitcast(F32).rearrange("p r (c u) -> p r c u", u=2)
+        pair_rows = 2 * block_rows
+        for pair in range(blocks_per_image // 2):
+            words = psum_words.tile([P, 2, 2 * P], F32)
+            for k in range(2):
+                by_half = last_nodes[:, 2 * pair + k, :].bitcast(F32).rearrange("p (q u) -> p u q", u=2)
+                for u in range(2):
+                    nc.tensor.transpose(words[:, u, k * P : (k + 1) * P], by_half[:, u, :], identity[:])
+            nc.scalar.copy(
+                out=framed_words[:, 1 + pair * pair_rows : 1 + (pair + 1) * pair_rows, 1 : W + 1, :],
+                in_=words[:].rearrange("p u (r c) -> p r c u", c=W),
+            )
+
+        sides = keep.tile([P, H, row_cols], F32)
+        for k in range(blocks_per_image):
+            r0 = k * block_rows
+            here = framed[:, 1 + r0 : 1 + r0 + block_rows, :]
+            nc.gpsimd.tensor_tensor(
+                out=sides[:, r0 : r0 + block_rows, :],
+                in0=here[:, :, 0:row_cols],
+                in1=here[:, :, 2 * PACK : 2 * PACK + row_cols],
+                op=ADD,
+            )
+            nc.gpsimd.tensor_tensor(
+                out=threes[:, 1 + r0 : 1 + r0 + block_rows, :],
+                in0=sides[:, r0 : r0 + block_rows, :],
+                in1=here[:, :, PACK : PACK + row_cols],
+                op=ADD,
+            )
+        for k in range(blocks_per_image):
+            r0 = k * block_rows
+            block = last_image * blocks_per_image + k
+            above_below = scratch.tile([P, block_rows, row_cols], F32)
+            nc.gpsimd.tensor_tensor(
+                out=above_below[:],
+                in0=threes[:, r0 : r0 + block_rows, :],
+                in1=threes[:, r0 + 2 : r0 + 2 + block_rows, :],
+                op=ADD,
+            )
+            nc.gpsimd.tensor_tensor(
+                out=grouped[:, block * word_cols : (block + 1) * word_cols].rearrange(
+                    "p (r x) -> p r x", x=row_cols
+                ),
+                in0=above_below[:],
+                in1=sides[:, r0 : r0 + block_rows, :],
+                op=ADD,
+            )
+
+        bias = keep.tile([P, outputs], F32)
+        nc.vector.tensor_copy(out=bias[:], in_=bias_bf16[:])
+
+        def sum_on_tensor_engine(block):
+            image, k = divmod(block, blocks_per_image)
+            sums = psum_sums.tile([P, PACK, P], F32)
+            for side in range(2):
+                i = 2 * k + side
+                place = 2 * i - window_start(i)
+                by_byte = windows_of[image][:, i, :].rearrange("p (q t) -> p t q", t=PACK)
+                for t in range(PACK):
+                    nc.tensor.matmul(
+                        out=sums[:, t, side * window_nodes_out : (side + 1) * window_nodes_out],
+                        lhsT=by_byte[:, t, :],
+                        rhs=adjacency[:, place, :, :].rearrange("p r c -> p (r c)"),
+                        start=True,
+                        stop=True,
+                    )
+            nc.scalar.copy(
+                out=grouped[:, block * word_cols : (block + 1) * word_cols].rearrange(
+                    "p (n t) -> p n t", t=PACK
+                ),
+                in_=sums[:].rearrange("p t n -> p n t"),
+            )
+
+        def quantise(first_block):
+            lo, hi = first_block, first_block + BLOCKS_PER_QUANTISE
+            nc.vector.quantize_mx(
+                out=codes[:, lo * P : hi * P].bitcast(FP8X4),
+                scales=scales[:, lo * P : hi * P],
+                in_=grouped[:, lo * word_cols : hi * word_cols],
+            )
+
+        def multiply(block):
+            result = results.tile([P, outputs], F32)
+            for n0 in range(0, outputs, BANK):
+                product = psum_out.tile([P, BANK], F32)
+                nc.tensor.matmul_mx(
+                    out=product[:],
+                    lhsT=codes[:, block * P : (block + 1) * P].bitcast(FP8X4),
+                    lhsT_scale=scales[:, block * P : (block + 1) * P],
+                    rhs=w_words[:, n0 : n0 + BANK].bitcast(FP8X4),
+                    rhs_scale=w_scales[:, n0 : n0 + BANK],
+                    start=True,
+                    stop=True,
+                )
+                nc.vector.tensor_tensor(
+                    out=result[:, n0 : n0 + BANK], in0=product[:], in1=bias[:, n0 : n0 + BANK], op=ADD
+                )
+            nc.sync.dma_start(out=out_rows[block * P : (block + 1) * P, :], in_=result[:])
+
+        summed_blocks = last_image * blocks_per_image
+        for first_block in range(0, blocks + BLOCKS_PER_QUANTISE, BLOCKS_PER_QUANTISE):
+            for block in range(first_block, first_block + BLOCKS_PER_QUANTISE):
+                if block < summed_blocks:
+                    sum_on_tensor_engine(block)
+            ready = first_block - BLOCKS_PER_QUANTISE
+            if ready >= 0:
+                quantise(ready)
+                for block in range(ready, ready + BLOCKS_PER_QUANTISE):
+                    multiply(block)

@@ -14,7 +14,8 @@ ADD = mybir.AluOpType.add
 P = 128
 PACK = 4
 BANK = 512
-BLOCKS_PER_QUANTISE = 2
+PAIR = 2
+SUMS_AHEAD = 12
 
 FLOPS = 2 * 4 * 1024 * 512 * 1024
 
@@ -24,52 +25,49 @@ def tile_graphconvlayer_kernel(tc, X, Wm_words, Wm_scales, b, H, W, out):
     images, nodes, features = X.shape
     outputs = b.shape[0]
     assert features == P * PACK, "one matmul_mx pass contracts all features"
-    assert nodes == H * W and P == 4 * W, "a block of 128 nodes is 4 rows of the grid"
-    block_rows = P // W
-    blocks_per_image = nodes // P
-    windows_per_image = 2 * blocks_per_image
+    assert nodes == H * W and P == 4 * W, "a slab of 128 nodes is 4 rows of the grid"
+    slab_rows = P // W
+    slabs_per_image = nodes // P
+    windows_per_image = 2 * slabs_per_image
     window_nodes_out = 2 * W
     last_image = images - 1
-    blocks = images * blocks_per_image
-    word_cols = P * PACK
+    slabs = images * slabs_per_image
+    slab_cols = P * PACK
+    row_cols = W * PACK
     out_rows = out.flatten_outer_dims()
 
     with ExitStack() as ctx:
         keep = ctx.enter_context(tc.tile_pool(name="keep", bufs=1))
-        scratch = ctx.enter_context(tc.tile_pool(name="scratch", bufs=2))
         results = ctx.enter_context(tc.tile_pool(name="results", bufs=6))
         psum_words = ctx.enter_context(tc.psum_pool(name="psum_words", bufs=2))
         psum_sums = ctx.enter_context(tc.psum_pool(name="psum_sums", bufs=2))
         psum_out = ctx.enter_context(tc.psum_pool(name="psum_out", bufs=4))
-
         ctx.enter_context(tc.manual_schedule())
 
-        w_scales = keep.tile([P, outputs], U8, align_bytes=64)
-        nc.vector.memset(w_scales[:].bitcast(I32), 0)
         framed = keep.tile([P, H + 2, (W + 2) * PACK], BF16)
         nc.vector.memset(framed[:].bitcast(F32), 0.0)
-        row_cols = W * PACK
         threes = keep.tile([P, H + 2, row_cols], F32)
         nc.vector.memset(threes[:, 0, :], 0.0)
         nc.vector.memset(threes[:, H + 1, :], 0.0)
+        w_scales = keep.tile([P, outputs], U8, align_bytes=64)
+        nc.vector.memset(w_scales[:].bitcast(I32), 0)
 
-        last_nodes = keep.tile([P, blocks_per_image, features], BF16)
-        nc.sync.dma_start(out=last_nodes[:], in_=X[last_image].rearrange("(k p) f -> p k f", p=P))
+        last_nodes = keep.tile([P, slabs_per_image, features], BF16)
+        for first in range(0, slabs_per_image, PAIR):
+            nc.sync.dma_start(
+                out=last_nodes[:, first : first + PAIR, :],
+                in_=X[last_image, first * P : (first + PAIR) * P, :].rearrange("(k p) f -> p k f", p=P),
+            )
         bias_bf16 = keep.tile([P, outputs], BF16)
         nc.scalar.dma_start(out=bias_bf16[:], in_=b.partition_broadcast(P))
-        for quadrant in range(4):
-            nc.sync.dma_start(
-                out=w_scales[32 * quadrant : 32 * quadrant + 4, :].bitcast(I32),
-                in_=Wm_scales[0, 4 * quadrant : 4 * quadrant + 4, :].bitcast(I32),
-            )
 
         def window_start(i):
-            return min(max(2 * i - 1, 0), H - block_rows)
+            return min(max(2 * i - 1, 0), H - slab_rows)
 
         def load_windows(image):
             windows = keep.tile([P, windows_per_image, features], BF16, name="windows%d" % image)
             rows = X[image]
-            inner = blocks_per_image - 1
+            inner = slabs_per_image - 1
             nc.sync.dma_start(out=windows[:, 0, :], in_=rows[0:P, :])
             for first in (1, 2):
                 start = window_start(first) * W
@@ -81,6 +79,11 @@ def tile_graphconvlayer_kernel(tc, X, Wm_words, Wm_scales, b, H, W, out):
             return windows
 
         windows_of = [load_windows(0)]
+        for quadrant in range(4):
+            nc.sync.dma_start(
+                out=w_scales[32 * quadrant : 32 * quadrant + 4, :].bitcast(I32),
+                in_=Wm_scales[0, 4 * quadrant : 4 * quadrant + 4, :].bitcast(I32),
+            )
         w_words = keep.tile([P, outputs], U32, align_bytes=64)
         nc.sync.dma_start(
             out=w_words[:].bitcast(I32), in_=Wm_words[0].rearrange("p n t -> p (n t)").bitcast(I32)
@@ -111,63 +114,63 @@ def tile_graphconvlayer_kernel(tc, X, Wm_words, Wm_scales, b, H, W, out):
         adjacency = keep.tile([P, 3, 2, W], BF16)
         nc.vector.tensor_copy(out=adjacency[:], in_=by_column[:].rearrange("p c a r -> p a r c"))
 
-        grouped = keep.tile([P, blocks * word_cols], BF16, align_bytes=64)
-        codes = keep.tile([P, blocks * P], U32, align_bytes=64)
-        scales = keep.tile([P, blocks * P], U8, align_bytes=64)
+        grouped = keep.tile([P, slabs * slab_cols], BF16, align_bytes=64)
+        codes = keep.tile([P, slabs * P], U32, align_bytes=64)
+        scales = keep.tile([P, slabs * P], U8, align_bytes=64)
 
         framed_words = framed[:].bitcast(F32).rearrange("p r (c u) -> p r c u", u=2)
-        pair_rows = 2 * block_rows
-        for pair in range(blocks_per_image // 2):
-            words = psum_words.tile([P, 2, 2 * P], F32)
-            for k in range(2):
-                by_half = last_nodes[:, 2 * pair + k, :].bitcast(F32).rearrange("p (q u) -> p u q", u=2)
+        pair_rows = PAIR * slab_rows
+        for r0 in range(0, H, pair_rows):
+            words = psum_words.tile([P, 2, PAIR * P], F32)
+            for k in range(PAIR):
+                slab_words = last_nodes[:, r0 // slab_rows + k, :].bitcast(F32)
+                by_half = slab_words.rearrange("p (q u) -> p u q", u=2)
                 for u in range(2):
                     nc.tensor.transpose(words[:, u, k * P : (k + 1) * P], by_half[:, u, :], identity[:])
             nc.scalar.copy(
-                out=framed_words[:, 1 + pair * pair_rows : 1 + (pair + 1) * pair_rows, 1 : W + 1, :],
+                out=framed_words[:, 1 + r0 : 1 + r0 + pair_rows, 1 : W + 1, :],
                 in_=words[:].rearrange("p u (r c) -> p r c u", c=W),
             )
 
         sides = keep.tile([P, H, row_cols], F32)
-        for k in range(blocks_per_image):
-            r0 = k * block_rows
-            here = framed[:, 1 + r0 : 1 + r0 + block_rows, :]
-            nc.gpsimd.tensor_tensor(
-                out=sides[:, r0 : r0 + block_rows, :],
-                in0=here[:, :, 0:row_cols],
-                in1=here[:, :, 2 * PACK : 2 * PACK + row_cols],
+        above_below = keep.tile([P, H, row_cols], F32)
+        last_grouped = grouped[:, last_image * slabs_per_image * slab_cols :].rearrange(
+            "p (r x) -> p r x", x=row_cols
+        )
+        for r0 in range(0, H, pair_rows):
+            nc.vector.tensor_tensor(
+                out=sides[:, r0 : r0 + pair_rows, :],
+                in0=framed[:, 1 + r0 : 1 + r0 + pair_rows, 0:row_cols],
+                in1=framed[:, 1 + r0 : 1 + r0 + pair_rows, 2 * PACK : 2 * PACK + row_cols],
                 op=ADD,
             )
-            nc.gpsimd.tensor_tensor(
-                out=threes[:, 1 + r0 : 1 + r0 + block_rows, :],
-                in0=sides[:, r0 : r0 + block_rows, :],
-                in1=here[:, :, PACK : PACK + row_cols],
+        for r0 in range(0, H, pair_rows):
+            nc.vector.tensor_tensor(
+                out=threes[:, 1 + r0 : 1 + r0 + pair_rows, :],
+                in0=sides[:, r0 : r0 + pair_rows, :],
+                in1=framed[:, 1 + r0 : 1 + r0 + pair_rows, PACK : PACK + row_cols],
                 op=ADD,
             )
-        for k in range(blocks_per_image):
-            r0 = k * block_rows
-            block = last_image * blocks_per_image + k
-            above_below = scratch.tile([P, block_rows, row_cols], F32)
-            nc.gpsimd.tensor_tensor(
-                out=above_below[:],
-                in0=threes[:, r0 : r0 + block_rows, :],
-                in1=threes[:, r0 + 2 : r0 + 2 + block_rows, :],
+        for r0 in range(0, H, pair_rows):
+            nc.vector.tensor_tensor(
+                out=above_below[:, r0 : r0 + pair_rows, :],
+                in0=threes[:, r0 : r0 + pair_rows, :],
+                in1=threes[:, r0 + 2 : r0 + 2 + pair_rows, :],
                 op=ADD,
             )
-            nc.gpsimd.tensor_tensor(
-                out=grouped[:, block * word_cols : (block + 1) * word_cols].rearrange(
-                    "p (r x) -> p r x", x=row_cols
-                ),
-                in0=above_below[:],
-                in1=sides[:, r0 : r0 + block_rows, :],
+        for r0 in range(0, H, pair_rows):
+            nc.vector.tensor_tensor(
+                out=last_grouped[:, r0 : r0 + pair_rows, :],
+                in0=above_below[:, r0 : r0 + pair_rows, :],
+                in1=sides[:, r0 : r0 + pair_rows, :],
                 op=ADD,
             )
 
         bias = keep.tile([P, outputs], F32)
         nc.vector.tensor_copy(out=bias[:], in_=bias_bf16[:])
 
-        def sum_on_tensor_engine(block):
-            image, k = divmod(block, blocks_per_image)
+        def sum_on_tensor_engine(slab):
+            image, k = divmod(slab, slabs_per_image)
             sums = psum_sums.tile([P, PACK, P], F32)
             for side in range(2):
                 i = 2 * k + side
@@ -182,28 +185,28 @@ def tile_graphconvlayer_kernel(tc, X, Wm_words, Wm_scales, b, H, W, out):
                         stop=True,
                     )
             nc.scalar.copy(
-                out=grouped[:, block * word_cols : (block + 1) * word_cols].rearrange(
+                out=grouped[:, slab * slab_cols : (slab + 1) * slab_cols].rearrange(
                     "p (n t) -> p n t", t=PACK
                 ),
                 in_=sums[:].rearrange("p t n -> p n t"),
             )
 
-        def quantise(first_block):
-            lo, hi = first_block, first_block + BLOCKS_PER_QUANTISE
+        def quantise(first_slab):
+            lo, hi = first_slab, first_slab + PAIR
             nc.vector.quantize_mx(
                 out=codes[:, lo * P : hi * P].bitcast(FP8X4),
                 scales=scales[:, lo * P : hi * P],
-                in_=grouped[:, lo * word_cols : hi * word_cols],
+                in_=grouped[:, lo * slab_cols : hi * slab_cols],
             )
 
-        def multiply(block):
+        def multiply(slab):
             result = results.tile([P, outputs], F32)
             for n0 in range(0, outputs, BANK):
                 product = psum_out.tile([P, BANK], F32)
                 nc.tensor.matmul_mx(
                     out=product[:],
-                    lhsT=codes[:, block * P : (block + 1) * P].bitcast(FP8X4),
-                    lhsT_scale=scales[:, block * P : (block + 1) * P],
+                    lhsT=codes[:, slab * P : (slab + 1) * P].bitcast(FP8X4),
+                    lhsT_scale=scales[:, slab * P : (slab + 1) * P],
                     rhs=w_words[:, n0 : n0 + BANK].bitcast(FP8X4),
                     rhs_scale=w_scales[:, n0 : n0 + BANK],
                     start=True,
@@ -212,15 +215,15 @@ def tile_graphconvlayer_kernel(tc, X, Wm_words, Wm_scales, b, H, W, out):
                 nc.vector.tensor_tensor(
                     out=result[:, n0 : n0 + BANK], in0=product[:], in1=bias[:, n0 : n0 + BANK], op=ADD
                 )
-            nc.sync.dma_start(out=out_rows[block * P : (block + 1) * P, :], in_=result[:])
+            nc.sync.dma_start(out=out_rows[slab * P : (slab + 1) * P, :], in_=result[:])
 
-        summed_blocks = last_image * blocks_per_image
-        for first_block in range(0, blocks + BLOCKS_PER_QUANTISE, BLOCKS_PER_QUANTISE):
-            for block in range(first_block, first_block + BLOCKS_PER_QUANTISE):
-                if block < summed_blocks:
-                    sum_on_tensor_engine(block)
-            ready = first_block - BLOCKS_PER_QUANTISE
-            if ready >= 0:
-                quantise(ready)
-                for block in range(ready, ready + BLOCKS_PER_QUANTISE):
-                    multiply(block)
+        summed_slabs = last_image * slabs_per_image
+        order = list(range(summed_slabs, slabs)) + list(range(summed_slabs))
+        for slab in range(SUMS_AHEAD):
+            sum_on_tensor_engine(slab)
+        for step in range(0, slabs, PAIR):
+            quantise(order[step])
+            for i in range(step, step + PAIR):
+                if SUMS_AHEAD + i < summed_slabs:
+                    sum_on_tensor_engine(SUMS_AHEAD + i)
+                multiply(order[i])

@@ -15,7 +15,7 @@ P = 128
 PACK = 4
 BANK = 512
 PAIR = 2
-SUMS_AHEAD = 12
+SUMS_AHEAD = 4
 
 FLOPS = 2 * 4 * 1024 * 512 * 1024
 
@@ -32,23 +32,46 @@ def tile_graphconvlayer_kernel(tc, X, Wm_words, Wm_scales, b, H, W, out):
     window_nodes_out = 2 * W
     last_image = images - 1
     slabs = images * slabs_per_image
+    summed_slabs = last_image * slabs_per_image
     slab_cols = P * PACK
-    row_cols = W * PACK
     out_rows = out.flatten_outer_dims()
 
     with ExitStack() as ctx:
         keep = ctx.enter_context(tc.tile_pool(name="keep", bufs=1))
-        results = ctx.enter_context(tc.tile_pool(name="results", bufs=6))
+        results = ctx.enter_context(tc.tile_pool(name="results", bufs=8))
         psum_words = ctx.enter_context(tc.psum_pool(name="psum_words", bufs=2))
         psum_sums = ctx.enter_context(tc.psum_pool(name="psum_sums", bufs=2))
         psum_out = ctx.enter_context(tc.psum_pool(name="psum_out", bufs=4))
         ctx.enter_context(tc.manual_schedule())
 
-        framed = keep.tile([P, H + 2, (W + 2) * PACK], BF16)
-        nc.vector.memset(framed[:].bitcast(F32), 0.0)
-        threes = keep.tile([P, H + 2, row_cols], F32)
-        nc.vector.memset(threes[:, 0, :], 0.0)
-        nc.vector.memset(threes[:, H + 1, :], 0.0)
+        def neighbour_sum(framed, rows, cell, result, label):
+            width = W * cell
+            sides = keep.tile([P, rows, width], F32, name=label + "_sides")
+            threes = keep.tile([P, rows + 2, width], F32, name=label + "_threes")
+            above_below = keep.tile([P, rows, width], F32, name=label + "_above_below")
+            nc.vector.memset(threes[:, 0, :], 0.0)
+            nc.vector.memset(threes[:, rows + 1, :], 0.0)
+
+            def add(engine, stage, r0, r1):
+                here = framed[:, 1 + r0 : 1 + r1, :]
+                target, in0, in1 = [
+                    (sides[:, r0:r1, :], here[:, :, 0:width], here[:, :, 2 * cell : 2 * cell + width]),
+                    (threes[:, 1 + r0 : 1 + r1, :], sides[:, r0:r1, :], here[:, :, cell : cell + width]),
+                    (above_below[:, r0:r1, :], threes[:, r0:r1, :], threes[:, 2 + r0 : 2 + r1, :]),
+                    (result[:, r0:r1, :], above_below[:, r0:r1, :], sides[:, r0:r1, :]),
+                ][stage]
+                engine.tensor_tensor(out=target, in0=in0, in1=in1, op=ADD)
+
+            return add
+
+        grouped = keep.tile([P, slabs * slab_cols], BF16, align_bytes=64)
+        codes = keep.tile([P, slabs * P], U32, align_bytes=64)
+        scales = keep.tile([P, slabs * P], U8, align_bytes=64)
+
+        framed_identity = keep.tile([P, slab_rows + 2, W + 2], BF16)
+        nc.vector.memset(framed_identity[:], 0.0)
+        framed_image = keep.tile([P, H + 2, (W + 2) * PACK], BF16)
+        nc.vector.memset(framed_image[:].bitcast(F32), 0.0)
         w_scales = keep.tile([P, outputs], U8, align_bytes=64)
         nc.vector.memset(w_scales[:].bitcast(I32), 0)
 
@@ -93,32 +116,16 @@ def tile_graphconvlayer_kernel(tc, X, Wm_words, Wm_scales, b, H, W, out):
 
         identity = keep.tile([P, P], F32)
         make_identity(nc, identity[:])
+        adjacency = keep.tile([P, slab_rows, W], BF16)
+        nc.vector.tensor_copy(
+            out=framed_identity[:, 1 : 1 + slab_rows, 1 : 1 + W],
+            in_=identity[:].rearrange("p (r c) -> p r c", c=W),
+        )
+        add_in_window = neighbour_sum(framed_identity, slab_rows, 1, adjacency, "window")
+        for stage in range(4):
+            add_in_window(nc.vector, stage, 0, slab_rows)
 
-        by_column = keep.tile([P, W, 3, 2], BF16)
-        nc.gpsimd.memset(by_column[:], 0.0)
-        for dr in (-1, 0, 1):
-            for dc in (-1, 0, 1):
-                if (dr, dc) != (0, 0):
-                    first = max(0, -dc)
-                    count = W - abs(dc)
-                    diagonal = by_column[:, first : first + count, :, :]
-                    nc.gpsimd.affine_select(
-                        out=diagonal,
-                        in_=diagonal,
-                        compare_op=mybir.AluOpType.not_equal,
-                        fill=1.0,
-                        base=-(W * dr + dc + first),
-                        channel_multiplier=1,
-                        pattern=[[-1, count], [-W, 3], [-W, 2]],
-                    )
-        adjacency = keep.tile([P, 3, 2, W], BF16)
-        nc.vector.tensor_copy(out=adjacency[:], in_=by_column[:].rearrange("p c a r -> p a r c"))
-
-        grouped = keep.tile([P, slabs * slab_cols], BF16, align_bytes=64)
-        codes = keep.tile([P, slabs * P], U32, align_bytes=64)
-        scales = keep.tile([P, slabs * P], U8, align_bytes=64)
-
-        framed_words = framed[:].bitcast(F32).rearrange("p r (c u) -> p r c u", u=2)
+        framed_words = framed_image[:].bitcast(F32).rearrange("p r (c u) -> p r c u", u=2)
         pair_rows = PAIR * slab_rows
         for r0 in range(0, H, pair_rows):
             words = psum_words.tile([P, 2, PAIR * P], F32)
@@ -132,39 +139,16 @@ def tile_graphconvlayer_kernel(tc, X, Wm_words, Wm_scales, b, H, W, out):
                 in_=words[:].rearrange("p u (r c) -> p r c u", c=W),
             )
 
-        sides = keep.tile([P, H, row_cols], F32)
-        above_below = keep.tile([P, H, row_cols], F32)
-        last_grouped = grouped[:, last_image * slabs_per_image * slab_cols :].rearrange(
-            "p (r x) -> p r x", x=row_cols
+        add_in_image = neighbour_sum(
+            framed_image,
+            H,
+            PACK,
+            grouped[:, summed_slabs * slab_cols :].rearrange("p (r x) -> p r x", x=W * PACK),
+            "image",
         )
-        for r0 in range(0, H, pair_rows):
-            nc.vector.tensor_tensor(
-                out=sides[:, r0 : r0 + pair_rows, :],
-                in0=framed[:, 1 + r0 : 1 + r0 + pair_rows, 0:row_cols],
-                in1=framed[:, 1 + r0 : 1 + r0 + pair_rows, 2 * PACK : 2 * PACK + row_cols],
-                op=ADD,
-            )
-        for r0 in range(0, H, pair_rows):
-            nc.vector.tensor_tensor(
-                out=threes[:, 1 + r0 : 1 + r0 + pair_rows, :],
-                in0=sides[:, r0 : r0 + pair_rows, :],
-                in1=framed[:, 1 + r0 : 1 + r0 + pair_rows, PACK : PACK + row_cols],
-                op=ADD,
-            )
-        for r0 in range(0, H, pair_rows):
-            nc.vector.tensor_tensor(
-                out=above_below[:, r0 : r0 + pair_rows, :],
-                in0=threes[:, r0 : r0 + pair_rows, :],
-                in1=threes[:, r0 + 2 : r0 + 2 + pair_rows, :],
-                op=ADD,
-            )
-        for r0 in range(0, H, pair_rows):
-            nc.vector.tensor_tensor(
-                out=last_grouped[:, r0 : r0 + pair_rows, :],
-                in0=above_below[:, r0 : r0 + pair_rows, :],
-                in1=sides[:, r0 : r0 + pair_rows, :],
-                op=ADD,
-            )
+        for stage in range(4):
+            for r0 in range(0, H, slab_rows):
+                add_in_image(nc.vector if stage == 0 else nc.gpsimd, stage, r0, r0 + slab_rows)
 
         bias = keep.tile([P, outputs], F32)
         nc.vector.tensor_copy(out=bias[:], in_=bias_bf16[:])
@@ -174,13 +158,13 @@ def tile_graphconvlayer_kernel(tc, X, Wm_words, Wm_scales, b, H, W, out):
             sums = psum_sums.tile([P, PACK, P], F32)
             for side in range(2):
                 i = 2 * k + side
-                place = 2 * i - window_start(i)
+                top = 2 * i - window_start(i)
                 by_byte = windows_of[image][:, i, :].rearrange("p (q t) -> p t q", t=PACK)
                 for t in range(PACK):
                     nc.tensor.matmul(
                         out=sums[:, t, side * window_nodes_out : (side + 1) * window_nodes_out],
                         lhsT=by_byte[:, t, :],
-                        rhs=adjacency[:, place, :, :].rearrange("p r c -> p (r c)"),
+                        rhs=adjacency[:, top : top + 2, :].rearrange("p r c -> p (r c)"),
                         start=True,
                         stop=True,
                     )
@@ -217,13 +201,11 @@ def tile_graphconvlayer_kernel(tc, X, Wm_words, Wm_scales, b, H, W, out):
                 )
             nc.sync.dma_start(out=out_rows[slab * P : (slab + 1) * P, :], in_=result[:])
 
-        summed_slabs = last_image * slabs_per_image
-        order = list(range(summed_slabs, slabs)) + list(range(summed_slabs))
         for slab in range(SUMS_AHEAD):
             sum_on_tensor_engine(slab)
-        for step in range(0, slabs, PAIR):
-            quantise(order[step])
-            for i in range(step, step + PAIR):
-                if SUMS_AHEAD + i < summed_slabs:
-                    sum_on_tensor_engine(SUMS_AHEAD + i)
-                multiply(order[i])
+        for first_slab in range(0, slabs, PAIR):
+            quantise(first_slab)
+            for slab in range(first_slab, first_slab + PAIR):
+                if slab + SUMS_AHEAD < summed_slabs:
+                    sum_on_tensor_engine(slab + SUMS_AHEAD)
+                multiply(slab)

@@ -201,10 +201,13 @@ def tile_graphconvlayer_kernel(tc, X, Wm_words, Wm_scales, b, H, W, out):
                 )
             nc.sync.dma_start(out=out_rows[slab * P : (slab + 1) * P, :], in_=result[:])
 
+        assert SUMS_AHEAD >= 2 * PAIR, "the pair that is quantised ahead must have been summed"
         for slab in range(SUMS_AHEAD):
             sum_on_tensor_engine(slab)
+        quantise(0)
         for first_slab in range(0, slabs, PAIR):
-            quantise(first_slab)
+            if first_slab + PAIR < slabs:
+                quantise(first_slab + PAIR)
             for slab in range(first_slab, first_slab + PAIR):
                 if slab + SUMS_AHEAD < summed_slabs:
                     sum_on_tensor_engine(slab + SUMS_AHEAD)

@@ -146,9 +146,14 @@ def tile_graphconvlayer_kernel(tc, X, Wm_words, Wm_scales, b, H, W, out):
             grouped[:, summed_slabs * slab_cols :].rearrange("p (r x) -> p r x", x=W * PACK),
             "image",
         )
-        for stage in range(4):
-            for r0 in range(0, H, slab_rows):
-                add_in_image(nc.vector if stage == 0 else nc.gpsimd, stage, r0, r0 + slab_rows)
+        for r0 in range(0, H, slab_rows):
+            add_in_image(nc.vector, 0, r0, r0 + slab_rows)
+        add_in_image(nc.gpsimd, 1, 0, slab_rows)
+        for r0 in range(0, H, slab_rows):
+            if r0 + slab_rows < H:
+                add_in_image(nc.gpsimd, 1, r0 + slab_rows, r0 + 2 * slab_rows)
+            add_in_image(nc.gpsimd, 2, r0, r0 + slab_rows)
+            add_in_image(nc.gpsimd, 3, r0, r0 + slab_rows)
 
         bias = keep.tile([P, outputs], F32)
         nc.vector.tensor_copy(out=bias[:], in_=bias_bf16[:])
@@ -201,13 +206,20 @@ def tile_graphconvlayer_kernel(tc, X, Wm_words, Wm_scales, b, H, W, out):
                 )
             nc.sync.dma_start(out=out_rows[slab * P : (slab + 1) * P, :], in_=result[:])
 
+        pairs_per_turn = summed_slabs // (slabs - summed_slabs)
+        order = []
+        for turn in range((slabs - summed_slabs) // PAIR):
+            for i in range(pairs_per_turn):
+                order.append((turn * pairs_per_turn + i) * PAIR)
+            order.append(summed_slabs + turn * PAIR)
+
         assert SUMS_AHEAD >= 2 * PAIR, "the pair that is quantised ahead must have been summed"
         for slab in range(SUMS_AHEAD):
             sum_on_tensor_engine(slab)
-        quantise(0)
-        for first_slab in range(0, slabs, PAIR):
-            if first_slab + PAIR < slabs:
-                quantise(first_slab + PAIR)
+        quantise(order[0])
+        for position, first_slab in enumerate(order):
+            if position + 1 < len(order):
+                quantise(order[position + 1])
             for slab in range(first_slab, first_slab + PAIR):
                 if slab + SUMS_AHEAD < summed_slabs:
                     sum_on_tensor_engine(slab + SUMS_AHEAD)

@@ -34,15 +34,78 @@ def tile_graphconvlayer_kernel(tc, X, Wm_words, Wm_scales, b, H, W, out):
     slabs = images * slabs_per_image
     summed_slabs = last_image * slabs_per_image
     slab_cols = P * PACK
+    b_rows_count = outputs // P
     out_rows = out.flatten_outer_dims()
 
     with ExitStack() as ctx:
         keep = ctx.enter_context(tc.tile_pool(name="keep", bufs=1))
         results = ctx.enter_context(tc.tile_pool(name="results", bufs=8))
-        psum_words = ctx.enter_context(tc.psum_pool(name="psum_words", bufs=2))
+        psum_early = ctx.enter_context(tc.psum_pool(name="psum_early", bufs=2))
         psum_sums = ctx.enter_context(tc.psum_pool(name="psum_sums", bufs=2))
         psum_out = ctx.enter_context(tc.psum_pool(name="psum_out", bufs=4))
         ctx.enter_context(tc.manual_schedule())
+
+        identity = keep.tile([P, P], F32)
+        adjacency = keep.tile([P, slab_rows, W], BF16)
+        framed_identity = keep.tile([P, slab_rows + 2, W + 2], BF16)
+        windows_of = [
+            keep.tile([P, windows_per_image, features], BF16, name="windows%d" % image)
+            for image in range(last_image)
+        ]
+        last_nodes = keep.tile([P, slabs_per_image, features], BF16)
+        framed_image = keep.tile([P, H + 2, (W + 2) * PACK], BF16)
+        grouped = keep.tile([P, slabs * slab_cols], BF16, align_bytes=64)
+        codes = keep.tile([P, slabs * P], U32, align_bytes=64)
+        scales = keep.tile([P, slabs * P], U8, align_bytes=64)
+        w_words = keep.tile([P, outputs], U32, align_bytes=64)
+        w_scales = keep.tile([P, outputs], U8, align_bytes=64)
+        b_rows_bf16 = keep.tile([P, P], BF16)
+        b_rows = keep.tile([P, P], F32)
+        b_upright = keep.tile([P, b_rows_count], F32)
+        b_repeated = keep.tile([P, b_rows_count, P], F32)
+        bias = keep.tile([P, outputs], F32)
+
+        def window_start(i):
+            return min(max(2 * i - 1, 0), H - slab_rows)
+
+        def load_window(image, i):
+            first_node = window_start(i) * W
+            nc.sync.dma_start(out=windows_of[image][:, i, :], in_=X[image, first_node : first_node + P, :])
+
+        def load_last_image():
+            for first in range(0, slabs_per_image, PAIR):
+                nc.sync.dma_start(
+                    out=last_nodes[:, first : first + PAIR, :],
+                    in_=X[last_image, first * P : (first + PAIR) * P, :].rearrange("(k p) f -> p k f", p=P),
+                )
+
+        def load_weight():
+            for quadrant in range(4):
+                nc.sync.dma_start(
+                    out=w_scales[32 * quadrant : 32 * quadrant + 4, :].bitcast(I32),
+                    in_=Wm_scales[0, 4 * quadrant : 4 * quadrant + 4, :].bitcast(I32),
+                )
+            nc.sync.dma_start(
+                out=w_words[:].bitcast(I32), in_=Wm_words[0].rearrange("p n t -> p (n t)").bitcast(I32)
+            )
+
+        def stand_b_up():
+            nc.vector.tensor_copy(out=b_rows[:], in_=b_rows_bf16[:])
+            upright = psum_early.tile([P, P], F32, tag="early")
+            nc.tensor.transpose(upright[:], b_rows[:], identity[:])
+            nc.scalar.copy(out=b_upright[:], in_=upright[:, 0:b_rows_count])
+
+        def repeat_b():
+            nc.vector.tensor_copy(
+                out=b_repeated[:], in_=b_upright[:].unsqueeze(2).to_broadcast([P, b_rows_count, P])
+            )
+
+        def lay_b_down():
+            for n0 in range(0, outputs, BANK):
+                spread = psum_early.tile([P, BANK], F32, tag="early")
+                for n in range(n0, n0 + BANK, P):
+                    nc.tensor.transpose(spread[:, n - n0 : n - n0 + P], b_repeated[:, n // P, :], identity[:])
+                nc.scalar.copy(out=bias[:, n0 : n0 + BANK], in_=spread[:])
 
         def neighbour_sum(framed, rows, cell, result, label):
             width = W * cell
@@ -64,99 +127,41 @@ def tile_graphconvlayer_kernel(tc, X, Wm_words, Wm_scales, b, H, W, out):
 
             return add
 
-        grouped = keep.tile([P, slabs * slab_cols], BF16, align_bytes=64)
-        codes = keep.tile([P, slabs * P], U32, align_bytes=64)
-        scales = keep.tile([P, slabs * P], U8, align_bytes=64)
-
-        framed_identity = keep.tile([P, slab_rows + 2, W + 2], BF16)
-        nc.vector.memset(framed_identity[:], 0.0)
-        framed_image = keep.tile([P, H + 2, (W + 2) * PACK], BF16)
-        nc.vector.memset(framed_image[:].bitcast(F32), 0.0)
-        w_scales = keep.tile([P, outputs], U8, align_bytes=64)
-        nc.vector.memset(w_scales[:].bitcast(I32), 0)
-
-        last_nodes = keep.tile([P, slabs_per_image, features], BF16)
-        for first in range(0, slabs_per_image, PAIR):
-            nc.sync.dma_start(
-                out=last_nodes[:, first : first + PAIR, :],
-                in_=X[last_image, first * P : (first + PAIR) * P, :].rearrange("(k p) f -> p k f", p=P),
+        def build_adjacency():
+            nc.vector.tensor_copy(
+                out=framed_identity[:, 1 : 1 + slab_rows, 1 : 1 + W],
+                in_=identity[:].rearrange("p (r c) -> p r c", c=W),
             )
-        bias_bf16 = keep.tile([P, outputs], BF16)
-        nc.scalar.dma_start(out=bias_bf16[:], in_=b.partition_broadcast(P))
+            add_in_window = neighbour_sum(framed_identity, slab_rows, 1, adjacency, "window")
+            for stage in range(4):
+                add_in_window(nc.vector, stage, 0, slab_rows)
 
-        def window_start(i):
-            return min(max(2 * i - 1, 0), H - slab_rows)
-
-        def load_windows(image):
-            windows = keep.tile([P, windows_per_image, features], BF16, name="windows%d" % image)
-            rows = X[image]
-            inner = slabs_per_image - 1
-            nc.sync.dma_start(out=windows[:, 0, :], in_=rows[0:P, :])
-            for first in (1, 2):
-                start = window_start(first) * W
-                nc.sync.dma_start(
-                    out=windows[:, first : first + 2 * inner : 2, :],
-                    in_=rows[start : start + inner * P, :].rearrange("(k p) f -> p k f", p=P),
+        def transpose_last_image():
+            framed_words = framed_image[:].bitcast(F32).rearrange("p r (c u) -> p r c u", u=2)
+            pair_rows = PAIR * slab_rows
+            for r0 in range(0, H, pair_rows):
+                words = psum_early.tile([P, 2, PAIR * P], F32, tag="early")
+                for k in range(PAIR):
+                    slab_words = last_nodes[:, r0 // slab_rows + k, :].bitcast(F32)
+                    by_half = slab_words.rearrange("p (q u) -> p u q", u=2)
+                    for u in range(2):
+                        nc.tensor.transpose(words[:, u, k * P : (k + 1) * P], by_half[:, u, :], identity[:])
+                nc.scalar.copy(
+                    out=framed_words[:, 1 + r0 : 1 + r0 + pair_rows, 1 : W + 1, :],
+                    in_=words[:].rearrange("p u (r c) -> p r c u", c=W),
                 )
-            nc.sync.dma_start(out=windows[:, windows_per_image - 1, :], in_=rows[nodes - P : nodes, :])
-            return windows
 
-        windows_of = [load_windows(0)]
-        for quadrant in range(4):
-            nc.sync.dma_start(
-                out=w_scales[32 * quadrant : 32 * quadrant + 4, :].bitcast(I32),
-                in_=Wm_scales[0, 4 * quadrant : 4 * quadrant + 4, :].bitcast(I32),
+        def add_last_image():
+            add_in_image = neighbour_sum(
+                framed_image,
+                H,
+                PACK,
+                grouped[:, summed_slabs * slab_cols :].rearrange("p (r x) -> p r x", x=W * PACK),
+                "image",
             )
-        w_words = keep.tile([P, outputs], U32, align_bytes=64)
-        nc.sync.dma_start(
-            out=w_words[:].bitcast(I32), in_=Wm_words[0].rearrange("p n t -> p (n t)").bitcast(I32)
-        )
-        for image in range(1, last_image):
-            windows_of.append(load_windows(image))
-
-        identity = keep.tile([P, P], F32)
-        make_identity(nc, identity[:])
-        adjacency = keep.tile([P, slab_rows, W], BF16)
-        nc.vector.tensor_copy(
-            out=framed_identity[:, 1 : 1 + slab_rows, 1 : 1 + W],
-            in_=identity[:].rearrange("p (r c) -> p r c", c=W),
-        )
-        add_in_window = neighbour_sum(framed_identity, slab_rows, 1, adjacency, "window")
-        for stage in range(4):
-            add_in_window(nc.vector, stage, 0, slab_rows)
-
-        framed_words = framed_image[:].bitcast(F32).rearrange("p r (c u) -> p r c u", u=2)
-        pair_rows = PAIR * slab_rows
-        for r0 in range(0, H, pair_rows):
-            words = psum_words.tile([P, 2, PAIR * P], F32)
-            for k in range(PAIR):
-                slab_words = last_nodes[:, r0 // slab_rows + k, :].bitcast(F32)
-                by_half = slab_words.rearrange("p (q u) -> p u q", u=2)
-                for u in range(2):
-                    nc.tensor.transpose(words[:, u, k * P : (k + 1) * P], by_half[:, u, :], identity[:])
-            nc.scalar.copy(
-                out=framed_words[:, 1 + r0 : 1 + r0 + pair_rows, 1 : W + 1, :],
-                in_=words[:].rearrange("p u (r c) -> p r c u", c=W),
-            )
-
-        add_in_image = neighbour_sum(
-            framed_image,
-            H,
-            PACK,
-            grouped[:, summed_slabs * slab_cols :].rearrange("p (r x) -> p r x", x=W * PACK),
-            "image",
-        )
-        for r0 in range(0, H, slab_rows):
-            add_in_image(nc.vector, 0, r0, r0 + slab_rows)
-        add_in_image(nc.gpsimd, 1, 0, slab_rows)
-        for r0 in range(0, H, slab_rows):
-            if r0 + slab_rows < H:
-                add_in_image(nc.gpsimd, 1, r0 + slab_rows, r0 + 2 * slab_rows)
-            add_in_image(nc.gpsimd, 2, r0, r0 + slab_rows)
-            add_in_image(nc.gpsimd, 3, r0, r0 + slab_rows)
-
-        bias = keep.tile([P, outputs], F32)
-        nc.vector.tensor_copy(out=bias[:], in_=bias_bf16[:])
+            for stage in range(4):
+                for r0 in range(0, H, slab_rows):
+                    add_in_image(nc.vector if stage == 0 else nc.gpsimd, stage, r0, r0 + slab_rows)
 
         def sum_on_tensor_engine(slab):
             image, k = divmod(slab, slabs_per_image)
@@ -206,20 +211,34 @@ def tile_graphconvlayer_kernel(tc, X, Wm_words, Wm_scales, b, H, W, out):
                 )
             nc.sync.dma_start(out=out_rows[slab * P : (slab + 1) * P, :], in_=result[:])
 
-        pairs_per_turn = summed_slabs // (slabs - summed_slabs)
-        order = []
-        for turn in range((slabs - summed_slabs) // PAIR):
-            for i in range(pairs_per_turn):
-                order.append((turn * pairs_per_turn + i) * PAIR)
-            order.append(summed_slabs + turn * PAIR)
+        nc.vector.memset(b_rows_bf16[:], 0.0)
+        nc.vector.memset(framed_identity[:], 0.0)
+        nc.vector.memset(framed_image[:].bitcast(F32), 0.0)
+        nc.vector.memset(w_scales[:].bitcast(I32), 0)
+
+        nc.sync.dma_start(out=b_rows_bf16[0:b_rows_count, :], in_=b.rearrange("(j n) -> j n", n=P))
+        load_last_image()
+        for image in range(last_image):
+            for i in range(windows_per_image):
+                if (image, i) == (0, 2 * SUMS_AHEAD):
+                    load_weight()
+                load_window(image, i)
+
+        make_identity(nc, identity[:])
+        stand_b_up()
+        build_adjacency()
+        repeat_b()
+        transpose_last_image()
+        lay_b_down()
+        add_last_image()
 
         assert SUMS_AHEAD >= 2 * PAIR, "the pair that is quantised ahead must have been summed"
         for slab in range(SUMS_AHEAD):
             sum_on_tensor_engine(slab)
-        quantise(order[0])
-        for position, first_slab in enumerate(order):
-            if position + 1 < len(order):
-                quantise(order[position + 1])
+        quantise(0)
+        for first_slab in range(0, slabs, PAIR):
+            if first_slab + PAIR < slabs:
+                quantise(first_slab + PAIR)
             for slab in range(first_slab, first_slab + PAIR):
                 if slab + SUMS_AHEAD < summed_slabs:
                     sum_on_tensor_engine(slab + SUMS_AHEAD)

@@ -39,7 +39,7 @@ def tile_graphconvlayer_kernel(tc, X, Wm_words, Wm_scales, b, H, W, out):
 
     with ExitStack() as ctx:
         keep = ctx.enter_context(tc.tile_pool(name="keep", bufs=1))
-        results = ctx.enter_context(tc.tile_pool(name="results", bufs=8))
+        results = ctx.enter_context(tc.tile_pool(name="results", bufs=5))
         psum_early = ctx.enter_context(tc.psum_pool(name="psum_early", bufs=2))
         psum_sums = ctx.enter_context(tc.psum_pool(name="psum_sums", bufs=2))
         psum_out = ctx.enter_context(tc.psum_pool(name="psum_out", bufs=4))
@@ -64,6 +64,13 @@ def tile_graphconvlayer_kernel(tc, X, Wm_words, Wm_scales, b, H, W, out):
         b_upright = keep.tile([P, b_rows_count], F32)
         b_repeated = keep.tile([P, b_rows_count, P], F32)
         bias = keep.tile([P, outputs], F32)
+
+        def parity_view(slab):
+            pair, half = divmod(slab, PAIR)
+            whole = grouped[:, pair * PAIR * slab_cols : (pair + 1) * PAIR * slab_cols].rearrange(
+                "p (e m t) -> p e m t", e=PAIR, t=PACK
+            )
+            return whole[:, :, half * (P // PAIR) : (half + 1) * (P // PAIR), :]
 
         def window_start(i):
             return min(max(2 * i - 1, 0), H - slab_rows)
@@ -107,7 +114,7 @@ def tile_graphconvlayer_kernel(tc, X, Wm_words, Wm_scales, b, H, W, out):
                     nc.tensor.transpose(spread[:, n - n0 : n - n0 + P], b_repeated[:, n // P, :], identity[:])
                 nc.scalar.copy(out=bias[:, n0 : n0 + BANK], in_=spread[:])
 
-        def neighbour_sum(framed, rows, cell, result, label):
+        def neighbour_sum(framed, rows, cell, result, label, by_parity=False, result_first_slab=0):
             width = W * cell
             sides = keep.tile([P, rows, width], F32, name=label + "_sides")
             threes = keep.tile([P, rows + 2, width], F32, name=label + "_threes")
@@ -123,6 +130,10 @@ def tile_graphconvlayer_kernel(tc, X, Wm_words, Wm_scales, b, H, W, out):
                     (above_below[:, r0:r1, :], threes[:, r0:r1, :], threes[:, 2 + r0 : 2 + r1, :]),
                     (result[:, r0:r1, :], above_below[:, r0:r1, :], sides[:, r0:r1, :]),
                 ][stage]
+                if stage == 3 and by_parity:
+                    in0 = in0.rearrange("p r (c e t) -> p e (r c) t", e=PAIR, t=cell)
+                    in1 = in1.rearrange("p r (c e t) -> p e (r c) t", e=PAIR, t=cell)
+                    target = parity_view(result_first_slab + r0 // slab_rows)
                 engine.tensor_tensor(out=target, in0=in0, in1=in1, op=ADD)
 
             return add
@@ -158,6 +169,8 @@ def tile_graphconvlayer_kernel(tc, X, Wm_words, Wm_scales, b, H, W, out):
                 PACK,
                 grouped[:, summed_slabs * slab_cols :].rearrange("p (r x) -> p r x", x=W * PACK),
                 "image",
+                by_parity=True,
+                result_first_slab=summed_slabs,
             )
             for stage in range(4):
                 for r0 in range(0, H, slab_rows):
@@ -178,12 +191,7 @@ def tile_graphconvlayer_kernel(tc, X, Wm_words, Wm_scales, b, H, W, out):
                         start=True,
                         stop=True,
                     )
-            nc.scalar.copy(
-                out=grouped[:, slab * slab_cols : (slab + 1) * slab_cols].rearrange(
-                    "p (n t) -> p n t", t=PACK
-                ),
-                in_=sums[:].rearrange("p t n -> p n t"),
-            )
+            nc.scalar.copy(out=parity_view(slab), in_=sums[:].rearrange("p t (m e) -> p e m t", e=PAIR))
 
         def quantise(first_slab):
             lo, hi = first_slab, first_slab + PAIR
@@ -193,8 +201,7 @@ def tile_graphconvlayer_kernel(tc, X, Wm_words, Wm_scales, b, H, W, out):
                 in_=grouped[:, lo * slab_cols : hi * slab_cols],
             )
 
-        def multiply(slab):
-            result = results.tile([P, outputs], F32)
+        def multiply(slab, result):
             for n0 in range(0, outputs, BANK):
                 product = psum_out.tile([P, BANK], F32)
                 nc.tensor.matmul_mx(
@@ -207,17 +214,16 @@ def tile_graphconvlayer_kernel(tc, X, Wm_words, Wm_scales, b, H, W, out):
                     stop=True,
                 )
                 nc.vector.tensor_tensor(
-                    out=result[:, n0 : n0 + BANK], in0=product[:], in1=bias[:, n0 : n0 + BANK], op=ADD
+                    out=result[:, slab % PAIR, n0 : n0 + BANK], in0=product[:], in1=bias[:, n0 : n0 + BANK], op=ADD
                 )
-            nc.sync.dma_start(out=out_rows[slab * P : (slab + 1) * P, :], in_=result[:])
 
         nc.vector.memset(b_rows_bf16[:], 0.0)
         nc.vector.memset(framed_identity[:], 0.0)
         nc.vector.memset(framed_image[:].bitcast(F32), 0.0)
         nc.vector.memset(w_scales[:].bitcast(I32), 0)
 
-        nc.sync.dma_start(out=b_rows_bf16[0:b_rows_count, :], in_=b.rearrange("(j n) -> j n", n=P))
         load_last_image()
+        nc.sync.dma_start(out=b_rows_bf16[0:b_rows_count, :], in_=b.rearrange("(j n) -> j n", n=P))
         for image in range(last_image):
             for i in range(windows_per_image):
                 if (image, i) == (0, 2 * SUMS_AHEAD):
@@ -239,7 +245,16 @@ def tile_graphconvlayer_kernel(tc, X, Wm_words, Wm_scales, b, H, W, out):
         for first_slab in range(0, slabs, PAIR):
             if first_slab + PAIR < slabs:
                 quantise(first_slab + PAIR)
+            result = results.tile([P, PAIR, outputs], F32)
+            pair_rows_of_out = out_rows[first_slab * P : (first_slab + PAIR) * P, :].rearrange(
+                "(m e) n -> m e n", e=PAIR
+            )
             for slab in range(first_slab, first_slab + PAIR):
                 if slab + SUMS_AHEAD < summed_slabs:
                     sum_on_tensor_engine(slab + SUMS_AHEAD)
-                multiply(slab)
+                multiply(slab, result)
+                if first_slab + PAIR == slabs:
+                    e = slab - first_slab
+                    nc.sync.dma_start(out=pair_rows_of_out[:, e, :], in_=result[:, e, :])
+            if first_slab + PAIR < slabs:
+                nc.sync.dma_start(out=pair_rows_of_out, in_=result[:])

@@ -60,9 +60,8 @@ def tile_graphconvlayer_kernel(tc, X, Wm_words, Wm_scales, b, H, W, out):
         w_words = keep.tile([P, outputs], U32, align_bytes=64)
         w_scales = keep.tile([P, outputs], U8, align_bytes=64)
         b_rows_bf16 = keep.tile([P, P], BF16)
-        b_rows = keep.tile([P, P], F32)
+        identity_bf16 = keep.tile([P, P], BF16)
         b_upright = keep.tile([P, b_rows_count], F32)
-        b_repeated = keep.tile([P, b_rows_count, P], F32)
         bias = keep.tile([P, outputs], F32)
 
         def parity_view(slab):
@@ -97,21 +96,19 @@ def tile_graphconvlayer_kernel(tc, X, Wm_words, Wm_scales, b, H, W, out):
             )
 
         def stand_b_up():
-            nc.vector.tensor_copy(out=b_rows[:], in_=b_rows_bf16[:])
-            upright = psum_early.tile([P, P], F32, tag="early")
-            nc.tensor.transpose(upright[:], b_rows[:], identity[:])
+            upright = psum_early.tile([P, P], BF16, tag="early")
+            nc.tensor.transpose(upright[:], b_rows_bf16[:], identity_bf16[:])
             nc.scalar.copy(out=b_upright[:], in_=upright[:, 0:b_rows_count])
-
-        def repeat_b():
-            nc.vector.tensor_copy(
-                out=b_repeated[:], in_=b_upright[:].unsqueeze(2).to_broadcast([P, b_rows_count, P])
-            )
 
         def lay_b_down():
             for n0 in range(0, outputs, BANK):
                 spread = psum_early.tile([P, BANK], F32, tag="early")
                 for n in range(n0, n0 + BANK, P):
-                    nc.tensor.transpose(spread[:, n - n0 : n - n0 + P], b_repeated[:, n // P, :], identity[:])
+                    nc.tensor.transpose(
+                        spread[:, n - n0 : n - n0 + P],
+                        b_upright[:, n // P : n // P + 1].to_broadcast([P, P]),
+                        identity[:],
+                    )
                 nc.scalar.copy(out=bias[:, n0 : n0 + BANK], in_=spread[:])
 
         def neighbour_sum(framed, rows, cell, result, label, by_parity=False, result_first_slab=0):
@@ -193,8 +190,8 @@ def tile_graphconvlayer_kernel(tc, X, Wm_words, Wm_scales, b, H, W, out):
                     )
             nc.scalar.copy(out=parity_view(slab), in_=sums[:].rearrange("p t (m e) -> p e m t", e=PAIR))
 
-        def quantise(first_slab):
-            lo, hi = first_slab, first_slab + PAIR
+        def quantise(first_slab, count):
+            lo, hi = first_slab, first_slab + count
             nc.vector.quantize_mx(
                 out=codes[:, lo * P : hi * P].bitcast(FP8X4),
                 scales=scales[:, lo * P : hi * P],
@@ -217,13 +214,14 @@ def tile_graphconvlayer_kernel(tc, X, Wm_words, Wm_scales, b, H, W, out):
                     out=result[:, slab % PAIR, n0 : n0 + BANK], in0=product[:], in1=bias[:, n0 : n0 + BANK], op=ADD
                 )
 
-        nc.vector.memset(b_rows_bf16[:], 0.0)
+        nc.gpsimd.memset(b_rows_bf16[:], 0.0)
         nc.vector.memset(framed_identity[:], 0.0)
-        nc.vector.memset(framed_image[:].bitcast(F32), 0.0)
+        nc.vector.memset(framed_image[:, :, 0:PACK], 0.0)
+        nc.vector.memset(framed_image[:, :, (W + 1) * PACK :], 0.0)
         nc.vector.memset(w_scales[:].bitcast(I32), 0)
 
-        load_last_image()
         nc.sync.dma_start(out=b_rows_bf16[0:b_rows_count, :], in_=b.rearrange("(j n) -> j n", n=P))
+        load_last_image()
         for image in range(last_image):
             for i in range(windows_per_image):
                 if (image, i) == (0, 2 * SUMS_AHEAD):
@@ -231,9 +229,9 @@ def tile_graphconvlayer_kernel(tc, X, Wm_words, Wm_scales, b, H, W, out):
                 load_window(image, i)
 
         make_identity(nc, identity[:])
+        make_identity(nc, identity_bf16[:])
         stand_b_up()
         build_adjacency()
-        repeat_b()
         transpose_last_image()
         lay_b_down()
         add_last_image()
@@ -241,17 +239,20 @@ def tile_graphconvlayer_kernel(tc, X, Wm_words, Wm_scales, b, H, W, out):
         assert SUMS_AHEAD >= 2 * PAIR, "the pair that is quantised ahead must have been summed"
         for slab in range(SUMS_AHEAD):
             sum_on_tensor_engine(slab)
-        quantise(0)
+        quantise(0, 2)
+        QUANTISE_AT = {0: (2, 2), 2: (4, 2), 4: (6, 2), 6: (8, 4), 10: (12, 4), 14: (16, 8), 22: (24, 4), 26: (28, 4)}
+        SUMS_BEFORE = {0: [4], 1: [5], 2: [6, 7], 3: [8], 4: [9, 10], 5: [11],
+                       10: [16, 17], 11: [18, 19], 12: [20, 21], 13: [22, 23]}
         for first_slab in range(0, slabs, PAIR):
-            if first_slab + PAIR < slabs:
-                quantise(first_slab + PAIR)
+            if first_slab in QUANTISE_AT:
+                quantise(*QUANTISE_AT[first_slab])
             result = results.tile([P, PAIR, outputs], F32)
             pair_rows_of_out = out_rows[first_slab * P : (first_slab + PAIR) * P, :].rearrange(
                 "(m e) n -> m e n", e=PAIR
             )
             for slab in range(first_slab, first_slab + PAIR):
-                if slab + SUMS_AHEAD < summed_slabs:
-                    sum_on_tensor_engine(slab + SUMS_AHEAD)
+                for summed in SUMS_BEFORE.get(slab, [slab + 6] if 6 <= slab < 10 else []):
+                    sum_on_tensor_engine(summed)
                 multiply(slab, result)
                 if first_slab + PAIR == slabs:
                     e = slab - first_slab

@@ -28,8 +28,9 @@ def tile_graphconvlayer_kernel(tc, X, Wm_words, Wm_scales, b, H, W, out):
     assert nodes == H * W and P == 4 * W, "a slab of 128 nodes is 4 rows of the grid"
     slab_rows = P // W
     slabs_per_image = nodes // P
-    windows_per_image = 2 * slabs_per_image
-    window_nodes_out = 2 * W
+    starts = [0] + list(range(slab_rows - 1, H - slab_rows - 2, 2)) + [H - slab_rows]
+    windows_per_image = len(starts)
+    below_row = slab_rows
     last_image = images - 1
     slabs = images * slabs_per_image
     summed_slabs = last_image * slabs_per_image
@@ -46,7 +47,7 @@ def tile_graphconvlayer_kernel(tc, X, Wm_words, Wm_scales, b, H, W, out):
         ctx.enter_context(tc.manual_schedule())
 
         identity = keep.tile([P, P], F32)
-        adjacency = keep.tile([P, slab_rows, W], BF16)
+        adjacency = keep.tile([P, slab_rows + 1, W], BF16)
         framed_identity = keep.tile([P, slab_rows + 2, W + 2], BF16)
         windows_of = [
             keep.tile([P, windows_per_image, features], BF16, name="windows%d" % image)
@@ -63,6 +64,8 @@ def tile_graphconvlayer_kernel(tc, X, Wm_words, Wm_scales, b, H, W, out):
         identity_bf16 = keep.tile([P, P], BF16)
         b_upright = keep.tile([P, b_rows_count], F32)
         bias = keep.tile([P, outputs], F32)
+        turned_slabs = range(16, 20)
+        turned = keep.tile([P, outputs // P, len(turned_slabs) * P], F32)
 
         def parity_view(slab):
             pair, half = divmod(slab, PAIR)
@@ -71,11 +74,8 @@ def tile_graphconvlayer_kernel(tc, X, Wm_words, Wm_scales, b, H, W, out):
             )
             return whole[:, :, half * (P // PAIR) : (half + 1) * (P // PAIR), :]
 
-        def window_start(i):
-            return min(max(2 * i - 1, 0), H - slab_rows)
-
         def load_window(image, i):
-            first_node = window_start(i) * W
+            first_node = starts[i] * W
             nc.sync.dma_start(out=windows_of[image][:, i, :], in_=X[image, first_node : first_node + P, :])
 
         def load_last_image():
@@ -133,16 +133,19 @@ def tile_graphconvlayer_kernel(tc, X, Wm_words, Wm_scales, b, H, W, out):
                     target = parity_view(result_first_slab + r0 // slab_rows)
                 engine.tensor_tensor(out=target, in0=in0, in1=in1, op=ADD)
 
-            return add
+            return add, threes
 
         def build_adjacency():
             nc.vector.tensor_copy(
                 out=framed_identity[:, 1 : 1 + slab_rows, 1 : 1 + W],
                 in_=identity[:].rearrange("p (r c) -> p r c", c=W),
             )
-            add_in_window = neighbour_sum(framed_identity, slab_rows, 1, adjacency, "window")
+            add_in_window, threes = neighbour_sum(
+                framed_identity, slab_rows, 1, adjacency[:, 0:slab_rows, :], "window"
+            )
             for stage in range(4):
                 add_in_window(nc.vector, stage, 0, slab_rows)
+            nc.vector.tensor_copy(out=adjacency[:, below_row, :], in_=threes[:, 1 + 2, :])
 
         def transpose_last_image():
             framed_words = framed_image[:].bitcast(F32).rearrange("p r (c u) -> p r c u", u=2)
@@ -160,7 +163,7 @@ def tile_graphconvlayer_kernel(tc, X, Wm_words, Wm_scales, b, H, W, out):
                 )
 
         def add_last_image():
-            add_in_image = neighbour_sum(
+            add_in_image, unused = neighbour_sum(
                 framed_image,
                 H,
                 PACK,
@@ -173,21 +176,38 @@ def tile_graphconvlayer_kernel(tc, X, Wm_words, Wm_scales, b, H, W, out):
                 for r0 in range(0, H, slab_rows):
                     add_in_image(nc.vector if stage == 0 else nc.gpsimd, stage, r0, r0 + slab_rows)
 
+        def row_pair_sums(r):
+            whole = {i: [row for row in (r, r + 1) if (row == 0 or row > starts[i]) and
+                         (row == H - 1 or row < starts[i] + slab_rows - 1)] for i in range(windows_per_image)}
+            for i in range(windows_per_image):
+                if starts[i] <= r and len(whole[i]) == 2:
+                    return [(r, 2, [(i, r - starts[i])])]
+            groups = []
+            for row in (r, r + 1):
+                complete = [i for i in range(windows_per_image) if row in whole[i]]
+                if complete:
+                    groups.append((row, 1, [(complete[0], row - starts[complete[0]])]))
+                else:
+                    lower = starts.index(row)
+                    groups.append((row, 1, [(lower - 1, below_row), (lower, 0)]))
+            return groups
+
         def sum_on_tensor_engine(slab):
             image, k = divmod(slab, slabs_per_image)
             sums = psum_sums.tile([P, PACK, P], F32)
-            for side in range(2):
-                i = 2 * k + side
-                top = 2 * i - window_start(i)
-                by_byte = windows_of[image][:, i, :].rearrange("p (q t) -> p t q", t=PACK)
+            for r in range(k * slab_rows, (k + 1) * slab_rows, 2):
                 for t in range(PACK):
-                    nc.tensor.matmul(
-                        out=sums[:, t, side * window_nodes_out : (side + 1) * window_nodes_out],
-                        lhsT=by_byte[:, t, :],
-                        rhs=adjacency[:, top : top + 2, :].rearrange("p r c -> p (r c)"),
-                        start=True,
-                        stop=True,
-                    )
+                    for row, count, parts in row_pair_sums(r):
+                        c0 = (row - k * slab_rows) * W
+                        for i, top in parts:
+                            by_byte = windows_of[image][:, i, :].rearrange("p (q t) -> p t q", t=PACK)
+                            nc.tensor.matmul(
+                                out=sums[:, t, c0 : c0 + count * W],
+                                lhsT=by_byte[:, t, :],
+                                rhs=adjacency[:, top : top + count, :].rearrange("p r c -> p (r c)"),
+                                start=(i, top) == parts[0],
+                                stop=(i, top) == parts[-1],
+                            )
             nc.scalar.copy(out=parity_view(slab), in_=sums[:].rearrange("p t (m e) -> p e m t", e=PAIR))
 
         def quantise(first_slab, count):
@@ -214,48 +234,88 @@ def tile_graphconvlayer_kernel(tc, X, Wm_words, Wm_scales, b, H, W, out):
                     out=result[:, slab % PAIR, n0 : n0 + BANK], in0=product[:], in1=bias[:, n0 : n0 + BANK], op=ADD
                 )
 
+        def multiply_turned(j):
+            product = psum_early.tile([P, BANK], F32, tag="early")
+            nc.tensor.matmul_mx(
+                out=product[:],
+                lhsT=w_words[:, j * P : (j + 1) * P].bitcast(FP8X4),
+                lhsT_scale=w_scales[:, j * P : (j + 1) * P],
+                rhs=codes[:, turned_slabs[0] * P : (turned_slabs[-1] + 1) * P].bitcast(FP8X4),
+                rhs_scale=scales[:, turned_slabs[0] * P : (turned_slabs[-1] + 1) * P],
+                start=True,
+                stop=True,
+            )
+            nc.scalar.activation(
+                out=turned[:, j, :],
+                in_=product[:],
+                func=mybir.ActivationFunctionType.Identity,
+                bias=b_upright[:, j : j + 1],
+            )
+
+        def turn_back(q, n0, result):
+            bank = psum_early.tile([P, BANK], F32, tag="early")
+            for n in range(n0, n0 + BANK, P):
+                nc.tensor.transpose(
+                    bank[:, n - n0 : n - n0 + P], turned[:, n // P, q * P : (q + 1) * P], identity[:]
+                )
+            nc.scalar.copy(out=result[:, q % PAIR, n0 : n0 + BANK], in_=bank[:])
+
         nc.gpsimd.memset(b_rows_bf16[:], 0.0)
         nc.vector.memset(framed_identity[:], 0.0)
         nc.vector.memset(framed_image[:, :, 0:PACK], 0.0)
         nc.vector.memset(framed_image[:, :, (W + 1) * PACK :], 0.0)
         nc.vector.memset(w_scales[:].bitcast(I32), 0)
 
-        nc.sync.dma_start(out=b_rows_bf16[0:b_rows_count, :], in_=b.rearrange("(j n) -> j n", n=P))
         load_last_image()
+        nc.sync.dma_start(out=b_rows_bf16[0:b_rows_count, :], in_=b.rearrange("(j n) -> j n", n=P))
         for image in range(last_image):
             for i in range(windows_per_image):
-                if (image, i) == (0, 2 * SUMS_AHEAD):
+                if (image, i) == (0, 2 * SUMS_AHEAD - 1):
                     load_weight()
                 load_window(image, i)
 
         make_identity(nc, identity[:])
         make_identity(nc, identity_bf16[:])
-        stand_b_up()
         build_adjacency()
         transpose_last_image()
-        lay_b_down()
+        stand_b_up()
         add_last_image()
 
-        assert SUMS_AHEAD >= 2 * PAIR, "the pair that is quantised ahead must have been summed"
-        for slab in range(SUMS_AHEAD):
+        for slab in range(PAIR):
             sum_on_tensor_engine(slab)
         quantise(0, 2)
-        QUANTISE_AT = {0: (2, 2), 2: (4, 2), 4: (6, 2), 6: (8, 4), 10: (12, 4), 14: (16, 8), 22: (24, 4), 26: (28, 4)}
-        SUMS_BEFORE = {0: [4], 1: [5], 2: [6, 7], 3: [8], 4: [9, 10], 5: [11],
+        lay_b_down()
+        sum_on_tensor_engine(2)
+        QUANTISE_AT = {1: (2, 2), 2: (4, 2), 4: (6, 2), 6: (8, 4), 10: (12, 4), 12: (16, 4), 15: (20, 4), 22: (24, 4), 26: (28, 4)}
+        SUMS_BEFORE = {1: [3, 4], 2: [5, 6], 3: [7, 8], 4: [9, 10], 5: [11],
                        10: [16, 17], 11: [18, 19], 12: [20, 21], 13: [22, 23]}
+        TURN_J = {14: [0, 1], 15: [2, 3], 20: [4, 5], 21: [6, 7]}
+        TURN_BACK = {22: [(0, 0), (0, 512)], 23: [(1, 0), (1, 512)], 24: [(2, 0)], 25: [(2, 512)], 26: [(3, 0)], 27: [(3, 512)]}
+
+        def out_of_pair(first_slab):
+            return out_rows[first_slab * P : (first_slab + PAIR) * P, :].rearrange("(m e) n -> m e n", e=PAIR)
+
         for first_slab in range(0, slabs, PAIR):
-            if first_slab in QUANTISE_AT:
-                quantise(*QUANTISE_AT[first_slab])
-            result = results.tile([P, PAIR, outputs], F32)
-            pair_rows_of_out = out_rows[first_slab * P : (first_slab + PAIR) * P, :].rearrange(
-                "(m e) n -> m e n", e=PAIR
-            )
+            if first_slab in turned_slabs:
+                continue
+            result = results.tile([P, PAIR, outputs], F32, tag="result")
             for slab in range(first_slab, first_slab + PAIR):
                 for summed in SUMS_BEFORE.get(slab, [slab + 6] if 6 <= slab < 10 else []):
                     sum_on_tensor_engine(summed)
+                if slab in QUANTISE_AT:
+                    quantise(*QUANTISE_AT[slab])
                 multiply(slab, result)
+                for j in TURN_J.get(slab, []):
+                    multiply_turned(j)
+                for q, n0 in TURN_BACK.get(slab, []):
+                    if q % PAIR == 0 and n0 == 0:
+                        turned_result = results.tile([P, PAIR, outputs], F32, tag="result")
+                    turn_back(q, n0, turned_result)
                 if first_slab + PAIR == slabs:
                     e = slab - first_slab
-                    nc.sync.dma_start(out=pair_rows_of_out[:, e, :], in_=result[:, e, :])
+                    nc.sync.dma_start(out=out_of_pair(first_slab)[:, e, :], in_=result[:, e, :])
             if first_slab + PAIR < slabs:
-                nc.sync.dma_start(out=pair_rows_of_out, in_=result[:])
+                nc.sync.dma_start(out=out_of_pair(first_slab), in_=result[:])
+            for q, n0 in TURN_BACK.get(first_slab + 1, []):
+                if (q % PAIR, n0) == (PAIR - 1, BANK):
+                    nc.sync.dma_start(out=out_of_pair(turned_slabs[q - 1]), in_=turned_result[:])

@@ -231,7 +231,7 @@ def tile_graphconvlayer_kernel(tc, X, Wm_words, Wm_scales, b, H, W, out):
                     stop=True,
                 )
                 nc.vector.tensor_tensor(
-                    out=result[:, slab % PAIR, n0 : n0 + BANK], in0=product[:], in1=bias[:, n0 : n0 + BANK], op=ADD
+                    out=result[:, slab % PAIR, n0 : n0 + BANK], in0=bias[:, n0 : n0 + BANK], in1=product[:], op=ADD
                 )
 
         def multiply_turned(j):

@@ -62,6 +62,7 @@ def tile_graphconvlayer_kernel(tc, X, Wm_words, Wm_scales, b, H, W, out):
         w_scales = keep.tile([P, outputs], U8, align_bytes=64)
         b_rows_bf16 = keep.tile([P, P], BF16)
         identity_bf16 = keep.tile([P, P], BF16)
+        b_upright_bf16 = keep.tile([P, b_rows_count], BF16)
         b_upright = keep.tile([P, b_rows_count], F32)
         bias = keep.tile([P, outputs], F32)
         turned_slabs = range(16, 20)
@@ -98,18 +99,16 @@ def tile_graphconvlayer_kernel(tc, X, Wm_words, Wm_scales, b, H, W, out):
         def stand_b_up():
             upright = psum_early.tile([P, P], BF16, tag="early")
             nc.tensor.transpose(upright[:], b_rows_bf16[:], identity_bf16[:])
+            nc.scalar.copy(out=b_upright_bf16[:], in_=upright[:, 0:b_rows_count])
             nc.scalar.copy(out=b_upright[:], in_=upright[:, 0:b_rows_count])
 
         def lay_b_down():
-            for n0 in range(0, outputs, BANK):
-                spread = psum_early.tile([P, BANK], F32, tag="early")
-                for n in range(n0, n0 + BANK, P):
-                    nc.tensor.transpose(
-                        spread[:, n - n0 : n - n0 + P],
-                        b_upright[:, n // P : n // P + 1].to_broadcast([P, P]),
-                        identity[:],
-                    )
-                nc.scalar.copy(out=bias[:, n0 : n0 + BANK], in_=spread[:])
+            spread = psum_early.tile([P, outputs], BF16, tag="early")
+            for n in range(0, outputs, P):
+                nc.tensor.transpose(
+                    spread[:, n : n + P], b_upright_bf16[:, n // P : n // P + 1].to_broadcast([P, P]), identity_bf16[:]
+                )
+            nc.scalar.copy(out=bias[:], in_=spread[:])
 
         def neighbour_sum(framed, rows, cell, result, label, by_parity=False, result_first_slab=0):
             width = W * cell
@@ -270,7 +269,7 @@ def tile_graphconvlayer_kernel(tc, X, Wm_words, Wm_scales, b, H, W, out):
         nc.sync.dma_start(out=b_rows_bf16[0:b_rows_count, :], in_=b.rearrange("(j n) -> j n", n=P))
         for image in range(last_image):
             for i in range(windows_per_image):
-                if (image, i) == (0, 2 * SUMS_AHEAD - 1):
+                if (image, i) == (0, 5):
                     load_weight()
                 load_window(image, i)
 
@@ -286,9 +285,9 @@ def tile_graphconvlayer_kernel(tc, X, Wm_words, Wm_scales, b, H, W, out):
         quantise(0, 2)
         lay_b_down()
         sum_on_tensor_engine(2)
-        QUANTISE_AT = {1: (2, 2), 2: (4, 2), 4: (6, 2), 6: (8, 4), 10: (12, 4), 12: (16, 4), 15: (20, 4), 22: (24, 4), 26: (28, 4)}
-        SUMS_BEFORE = {1: [3, 4], 2: [5, 6], 3: [7, 8], 4: [9, 10], 5: [11],
-                       10: [16, 17], 11: [18, 19], 12: [20, 21], 13: [22, 23]}
+        QUANTISE_AT = {1: (2, 2), 2: (4, 2), 4: (6, 2), 6: (8, 4), 10: (12, 4), 13: (16, 4), 15: (20, 4), 22: (24, 4), 26: (28, 4)}
+        SUMS_BEFORE = {1: [3, 4], 2: [5, 6], 3: [7], 4: [8, 9], 5: [10, 11],
+                       10: [16], 11: [17, 18], 12: [19, 20], 13: [21, 22], 14: [23]}
         TURN_J = {14: [0, 1], 15: [2, 3], 20: [4, 5], 21: [6, 7]}
         TURN_BACK = {22: [(0, 0), (0, 512)], 23: [(1, 0), (1, 512)], 24: [(2, 0)], 25: [(2, 512)], 26: [(3, 0)], 27: [(3, 512)]}
 

@@ -173,7 +173,8 @@ def tile_graphconvlayer_kernel(tc, X, Wm_words, Wm_scales, b, H, W, out):
             )
             for stage in range(4):
                 for r0 in range(0, H, slab_rows):
-                    add_in_image(nc.vector if stage == 0 else nc.gpsimd, stage, r0, r0 + slab_rows)
+                    by_vector = stage == 0 or stage == 1 and r0 < H // 2
+                    add_in_image(nc.vector if by_vector else nc.gpsimd, stage, r0, r0 + slab_rows)
 
         def row_pair_sums(r):
             whole = {i: [row for row in (r, r + 1) if (row == 0 or row > starts[i]) and

@@ -161,7 +161,7 @@ def tile_graphconvlayer_kernel(tc, X, Wm_words, Wm_scales, b, H, W, out):
                     in_=words[:].rearrange("p u (r c) -> p r c u", c=W),
                 )
 
-        def add_last_image():
+        def last_image_adder():
             add_in_image, unused = neighbour_sum(
                 framed_image,
                 H,
@@ -171,10 +171,11 @@ def tile_graphconvlayer_kernel(tc, X, Wm_words, Wm_scales, b, H, W, out):
                 by_parity=True,
                 result_first_slab=summed_slabs,
             )
-            for stage in range(4):
-                for r0 in range(0, H, slab_rows):
-                    by_vector = stage == 0 or stage == 1 and r0 < H // 2
-                    add_in_image(nc.vector if by_vector else nc.gpsimd, stage, r0, r0 + slab_rows)
+            def add_slabs(engine, stage, first, last):
+                for k in range(first, last):
+                    add_in_image(engine, stage, k * slab_rows, (k + 1) * slab_rows)
+
+            return add_slabs
 
         def row_pair_sums(r):
             whole = {i: [row for row in (r, r + 1) if (row == 0 or row > starts[i]) and
@@ -279,11 +280,14 @@ def tile_graphconvlayer_kernel(tc, X, Wm_words, Wm_scales, b, H, W, out):
         build_adjacency()
         transpose_last_image()
         stand_b_up()
-        add_last_image()
+        add_slabs = last_image_adder()
+        add_slabs(nc.vector, 0, 0, slabs_per_image)
+        add_slabs(nc.gpsimd, 1, 0, slabs_per_image // 2)
 
         for slab in range(PAIR):
             sum_on_tensor_engine(slab)
         quantise(0, 2)
+        add_slabs(nc.vector, 1, slabs_per_image // 2, slabs_per_image // 2 + PAIR)
         lay_b_down()
         sum_on_tensor_engine(2)
         QUANTISE_AT = {1: (2, 2), 2: (4, 2), 4: (6, 2), 6: (8, 4), 10: (12, 4), 13: (16, 4), 15: (20, 4), 22: (24, 4), 26: (28, 4)}
@@ -305,6 +309,12 @@ def tile_graphconvlayer_kernel(tc, X, Wm_words, Wm_scales, b, H, W, out):
                 if slab in QUANTISE_AT:
                     quantise(*QUANTISE_AT[slab])
                 multiply(slab, result)
+                if slab < 2:
+                    k = slabs_per_image // 2 + PAIR + slab
+                    add_slabs(nc.vector, 1, k, k + 1)
+                if slab == 1:
+                    for stage in (2, 3):
+                        add_slabs(nc.gpsimd, stage, 0, slabs_per_image)
                 for j in TURN_J.get(slab, []):
                     multiply_turned(j)
                 for q, n0 in TURN_BACK.get(slab, []):

from contextlib import ExitStack

import concourse.mybir as mybir
from concourse.masks import make_identity

F32 = mybir.dt.float32
BF16 = mybir.dt.bfloat16
I32 = mybir.dt.int32
U32 = mybir.dt.uint32
U8 = mybir.dt.uint8
FP8X4 = mybir.dt.float8_e4m3fn_x4
ADD = mybir.AluOpType.add

P = 128
PACK = 4
BANK = 512
PAIR = 2
SUMS_AHEAD = 4

FLOPS = 2 * 4 * 1024 * 512 * 1024


def tile_graphconvlayer_kernel(tc, X, Wm_words, Wm_scales, b, H, W, out):
    nc = tc.nc
    images, nodes, features = X.shape
    outputs = b.shape[0]
    assert features == P * PACK, "one matmul_mx pass contracts all features"
    assert nodes == H * W and P == 4 * W, "a slab of 128 nodes is 4 rows of the grid"
    slab_rows = P // W
    slabs_per_image = nodes // P
    starts = [0] + list(range(slab_rows - 1, H - slab_rows - 2, 2)) + [H - slab_rows]
    windows_per_image = len(starts)
    below_row = slab_rows
    last_image = images - 1
    slabs = images * slabs_per_image
    summed_slabs = last_image * slabs_per_image
    slab_cols = P * PACK
    b_rows_count = outputs // P
    out_rows = out.flatten_outer_dims()

    with ExitStack() as ctx:
        keep = ctx.enter_context(tc.tile_pool(name="keep", bufs=1))
        results = ctx.enter_context(tc.tile_pool(name="results", bufs=5))
        psum_early = ctx.enter_context(tc.psum_pool(name="psum_early", bufs=2))
        psum_sums = ctx.enter_context(tc.psum_pool(name="psum_sums", bufs=2))
        psum_out = ctx.enter_context(tc.psum_pool(name="psum_out", bufs=4))
        ctx.enter_context(tc.manual_schedule())

        identity = keep.tile([P, P], F32)
        adjacency = keep.tile([P, slab_rows + 1, W], BF16)
        framed_identity = keep.tile([P, slab_rows + 2, W + 2], BF16)
        windows_of = [
            keep.tile([P, windows_per_image, features], BF16, name="windows%d" % image)
            for image in range(last_image)
        ]
        last_nodes = keep.tile([P, slabs_per_image, features], BF16)
        framed_image = keep.tile([P, H + 2, (W + 2) * PACK], BF16)
        grouped = keep.tile([P, slabs * slab_cols], BF16, align_bytes=64)
        codes = keep.tile([P, slabs * P], U32, align_bytes=64)
        scales = keep.tile([P, slabs * P], U8, align_bytes=64)
        w_words = keep.tile([P, outputs], U32, align_bytes=64)
        w_scales = keep.tile([P, outputs], U8, align_bytes=64)
        b_rows_bf16 = keep.tile([P, P], BF16)
        identity_bf16 = keep.tile([P, P], BF16)
        b_upright_bf16 = keep.tile([P, b_rows_count], BF16)
        b_upright = keep.tile([P, b_rows_count], F32)
        bias = keep.tile([P, outputs], F32)
        turned_slabs = range(16, 20)
        turned = keep.tile([P, outputs // P, len(turned_slabs) * P], F32)

        def parity_view(slab):
            pair, half = divmod(slab, PAIR)
            whole = grouped[:, pair * PAIR * slab_cols : (pair + 1) * PAIR * slab_cols].rearrange(
                "p (e m t) -> p e m t", e=PAIR, t=PACK
            )
            return whole[:, :, half * (P // PAIR) : (half + 1) * (P // PAIR), :]

        def load_window(image, i):
            first_node = starts[i] * W
            nc.sync.dma_start(out=windows_of[image][:, i, :], in_=X[image, first_node : first_node + P, :])

        def load_last_image():
            for first in range(0, slabs_per_image, PAIR):
                nc.sync.dma_start(
                    out=last_nodes[:, first : first + PAIR, :],
                    in_=X[last_image, first * P : (first + PAIR) * P, :].rearrange("(k p) f -> p k f", p=P),
                )

        def load_weight():
            for quadrant in range(4):
                nc.sync.dma_start(
                    out=w_scales[32 * quadrant : 32 * quadrant + 4, :].bitcast(I32),
                    in_=Wm_scales[0, 4 * quadrant : 4 * quadrant + 4, :].bitcast(I32),
                )
            nc.sync.dma_start(
                out=w_words[:].bitcast(I32), in_=Wm_words[0].rearrange("p n t -> p (n t)").bitcast(I32)
            )

        def stand_b_up():
            upright = psum_early.tile([P, P], BF16, tag="early")
            nc.tensor.transpose(upright[:], b_rows_bf16[:], identity_bf16[:])
            nc.scalar.copy(out=b_upright_bf16[:], in_=upright[:, 0:b_rows_count])
            nc.scalar.copy(out=b_upright[:], in_=upright[:, 0:b_rows_count])

        def lay_b_down():
            spread = psum_early.tile([P, outputs], BF16, tag="early")
            for n in range(0, outputs, P):
                nc.tensor.transpose(
                    spread[:, n : n + P], b_upright_bf16[:, n // P : n // P + 1].to_broadcast([P, P]), identity_bf16[:]
                )
            nc.scalar.copy(out=bias[:], in_=spread[:])

        def neighbour_sum(framed, rows, cell, result, label, by_parity=False, result_first_slab=0):
            width = W * cell
            sides = keep.tile([P, rows, width], F32, name=label + "_sides")
            threes = keep.tile([P, rows + 2, width], F32, name=label + "_threes")
            above_below = keep.tile([P, rows, width], F32, name=label + "_above_below")
            nc.vector.memset(threes[:, 0, :], 0.0)
            nc.vector.memset(threes[:, rows + 1, :], 0.0)

            def add(engine, stage, r0, r1):
                here = framed[:, 1 + r0 : 1 + r1, :]
                target, in0, in1 = [
                    (sides[:, r0:r1, :], here[:, :, 0:width], here[:, :, 2 * cell : 2 * cell + width]),
                    (threes[:, 1 + r0 : 1 + r1, :], sides[:, r0:r1, :], here[:, :, cell : cell + width]),
                    (above_below[:, r0:r1, :], threes[:, r0:r1, :], threes[:, 2 + r0 : 2 + r1, :]),
                    (result[:, r0:r1, :], above_below[:, r0:r1, :], sides[:, r0:r1, :]),
                ][stage]
                if stage == 3 and by_parity:
                    in0 = in0.rearrange("p r (c e t) -> p e (r c) t", e=PAIR, t=cell)
                    in1 = in1.rearrange("p r (c e t) -> p e (r c) t", e=PAIR, t=cell)
                    target = parity_view(result_first_slab + r0 // slab_rows)
                engine.tensor_tensor(out=target, in0=in0, in1=in1, op=ADD)

            return add, threes

        def build_adjacency():
            nc.vector.tensor_copy(
                out=framed_identity[:, 1 : 1 + slab_rows, 1 : 1 + W],
                in_=identity[:].rearrange("p (r c) -> p r c", c=W),
            )
            add_in_window, threes = neighbour_sum(
                framed_identity, slab_rows, 1, adjacency[:, 0:slab_rows, :], "window"
            )
            for stage in range(4):
                add_in_window(nc.vector, stage, 0, slab_rows)
            nc.vector.tensor_copy(out=adjacency[:, below_row, :], in_=threes[:, 1 + 2, :])

        def transpose_last_image():
            framed_words = framed_image[:].bitcast(F32).rearrange("p r (c u) -> p r c u", u=2)
            pair_rows = PAIR * slab_rows
            for r0 in range(0, H, pair_rows):
                words = psum_early.tile([P, 2, PAIR * P], F32, tag="early")
                for k in range(PAIR):
                    slab_words = last_nodes[:, r0 // slab_rows + k, :].bitcast(F32)
                    by_half = slab_words.rearrange("p (q u) -> p u q", u=2)
                    for u in range(2):
                        nc.tensor.transpose(words[:, u, k * P : (k + 1) * P], by_half[:, u, :], identity[:])
                nc.scalar.copy(
                    out=framed_words[:, 1 + r0 : 1 + r0 + pair_rows, 1 : W + 1, :],
                    in_=words[:].rearrange("p u (r c) -> p r c u", c=W),
                )

        def last_image_adder():
            add_in_image, unused = neighbour_sum(
                framed_image,
                H,
                PACK,
                grouped[:, summed_slabs * slab_cols :].rearrange("p (r x) -> p r x", x=W * PACK),
                "image",
                by_parity=True,
                result_first_slab=summed_slabs,
            )
            def add_slabs(engine, stage, first, last):
                for k in range(first, last):
                    add_in_image(engine, stage, k * slab_rows, (k + 1) * slab_rows)

            return add_slabs

        def row_pair_sums(r):
            whole = {i: [row for row in (r, r + 1) if (row == 0 or row > starts[i]) and
                         (row == H - 1 or row < starts[i] + slab_rows - 1)] for i in range(windows_per_image)}
            for i in range(windows_per_image):
                if starts[i] <= r and len(whole[i]) == 2:
                    return [(r, 2, [(i, r - starts[i])])]
            groups = []
            for row in (r, r + 1):
                complete = [i for i in range(windows_per_image) if row in whole[i]]
                if complete:
                    groups.append((row, 1, [(complete[0], row - starts[complete[0]])]))
                else:
                    lower = starts.index(row)
                    groups.append((row, 1, [(lower - 1, below_row), (lower, 0)]))
            return groups

        def sum_on_tensor_engine(slab):
            image, k = divmod(slab, slabs_per_image)
            sums = psum_sums.tile([P, PACK, P], F32)
            for r in range(k * slab_rows, (k + 1) * slab_rows, 2):
                for t in range(PACK):
                    for row, count, parts in row_pair_sums(r):
                        c0 = (row - k * slab_rows) * W
                        for i, top in parts:
                            by_byte = windows_of[image][:, i, :].rearrange("p (q t) -> p t q", t=PACK)
                            nc.tensor.matmul(
                                out=sums[:, t, c0 : c0 + count * W],
                                lhsT=by_byte[:, t, :],
                                rhs=adjacency[:, top : top + count, :].rearrange("p r c -> p (r c)"),
                                start=(i, top) == parts[0],
                                stop=(i, top) == parts[-1],
                            )
            nc.scalar.copy(out=parity_view(slab), in_=sums[:].rearrange("p t (m e) -> p e m t", e=PAIR))

        def quantise(first_slab, count):
            lo, hi = first_slab, first_slab + count
            nc.vector.quantize_mx(
                out=codes[:, lo * P : hi * P].bitcast(FP8X4),
                scales=scales[:, lo * P : hi * P],
                in_=grouped[:, lo * slab_cols : hi * slab_cols],
            )

        def multiply(slab, result):
            for n0 in range(0, outputs, BANK):
                product = psum_out.tile([P, BANK], F32)
                nc.tensor.matmul_mx(
                    out=product[:],
                    lhsT=codes[:, slab * P : (slab + 1) * P].bitcast(FP8X4),
                    lhsT_scale=scales[:, slab * P : (slab + 1) * P],
                    rhs=w_words[:, n0 : n0 + BANK].bitcast(FP8X4),
                    rhs_scale=w_scales[:, n0 : n0 + BANK],
                    start=True,
                    stop=True,
                )
                nc.vector.tensor_tensor(
                    out=result[:, slab % PAIR, n0 : n0 + BANK], in0=bias[:, n0 : n0 + BANK], in1=product[:], op=ADD
                )

        def multiply_turned(j):
            product = psum_early.tile([P, BANK], F32, tag="early")
            nc.tensor.matmul_mx(
                out=product[:],
                lhsT=w_words[:, j * P : (j + 1) * P].bitcast(FP8X4),
                lhsT_scale=w_scales[:, j * P : (j + 1) * P],
                rhs=codes[:, turned_slabs[0] * P : (turned_slabs[-1] + 1) * P].bitcast(FP8X4),
                rhs_scale=scales[:, turned_slabs[0] * P : (turned_slabs[-1] + 1) * P],
                start=True,
                stop=True,
            )
            nc.scalar.activation(
                out=turned[:, j, :],
                in_=product[:],
                func=mybir.ActivationFunctionType.Identity,
                bias=b_upright[:, j : j + 1],
            )

        def turn_back(q, n0, result):
            bank = psum_early.tile([P, BANK], F32, tag="early")
            for n in range(n0, n0 + BANK, P):
                nc.tensor.transpose(
                    bank[:, n - n0 : n - n0 + P], turned[:, n // P, q * P : (q + 1) * P], identity[:]
                )
            nc.scalar.copy(out=result[:, q % PAIR, n0 : n0 + BANK], in_=bank[:])

        nc.gpsimd.memset(b_rows_bf16[:], 0.0)
        nc.vector.memset(framed_identity[:], 0.0)
        nc.vector.memset(framed_image[:, :, 0:PACK], 0.0)
        nc.vector.memset(framed_image[:, :, (W + 1) * PACK :], 0.0)
        nc.vector.memset(w_scales[:].bitcast(I32), 0)

        load_last_image()
        nc.sync.dma_start(out=b_rows_bf16[0:b_rows_count, :], in_=b.rearrange("(j n) -> j n", n=P))
        for image in range(last_image):
            for i in range(windows_per_image):
                if (image, i) == (0, 5):
                    load_weight()
                load_window(image, i)

        make_identity(nc, identity[:])
        make_identity(nc, identity_bf16[:])
        build_adjacency()
        transpose_last_image()
        stand_b_up()
        add_slabs = last_image_adder()
        add_slabs(nc.vector, 0, 0, slabs_per_image)
        add_slabs(nc.gpsimd, 1, 0, slabs_per_image // 2)

        for slab in range(PAIR):
            sum_on_tensor_engine(slab)
        quantise(0, 2)
        add_slabs(nc.vector, 1, slabs_per_image // 2, slabs_per_image // 2 + PAIR)
        lay_b_down()
        sum_on_tensor_engine(2)
        QUANTISE_AT = {1: (2, 2), 2: (4, 2), 4: (6, 2), 6: (8, 4), 10: (12, 4), 13: (16, 4), 15: (20, 4), 22: (24, 4), 26: (28, 4)}
        SUMS_BEFORE = {1: [3, 4], 2: [5, 6], 3: [7], 4: [8, 9], 5: [10, 11],
                       10: [16], 11: [17, 18], 12: [19, 20], 13: [21, 22], 14: [23]}
        TURN_J = {14: [0, 1], 15: [2, 3], 20: [4, 5], 21: [6, 7]}
        TURN_BACK = {22: [(0, 0), (0, 512)], 23: [(1, 0), (1, 512)], 24: [(2, 0)], 25: [(2, 512)], 26: [(3, 0)], 27: [(3, 512)]}

        def out_of_pair(first_slab):
            return out_rows[first_slab * P : (first_slab + PAIR) * P, :].rearrange("(m e) n -> m e n", e=PAIR)

        for first_slab in range(0, slabs, PAIR):
            if first_slab in turned_slabs:
                continue
            result = results.tile([P, PAIR, outputs], F32, tag="result")
            for slab in range(first_slab, first_slab + PAIR):
                for summed in SUMS_BEFORE.get(slab, [slab + 6] if 6 <= slab < 10 else []):
                    sum_on_tensor_engine(summed)
                if slab in QUANTISE_AT:
                    quantise(*QUANTISE_AT[slab])
                multiply(slab, result)
                if slab < 2:
                    k = slabs_per_image // 2 + PAIR + slab
                    add_slabs(nc.vector, 1, k, k + 1)
                if slab == 1:
                    for stage in (2, 3):
                        add_slabs(nc.gpsimd, stage, 0, slabs_per_image)
                for j in TURN_J.get(slab, []):
                    multiply_turned(j)
                for q, n0 in TURN_BACK.get(slab, []):
                    if q % PAIR == 0 and n0 == 0:
                        turned_result = results.tile([P, PAIR, outputs], F32, tag="result")
                    turn_back(q, n0, turned_result)
                if first_slab + PAIR == slabs:
                    e = slab - first_slab
                    nc.sync.dma_start(out=out_of_pair(first_slab)[:, e, :], in_=result[:, e, :])
            if first_slab + PAIR < slabs:
                nc.sync.dma_start(out=out_of_pair(first_slab), in_=result[:])
            for q, n0 in TURN_BACK.get(first_slab + 1, []):
                if (q % PAIR, n0) == (PAIR - 1, BANK):
                    nc.sync.dma_start(out=out_of_pair(turned_slabs[q - 1]), in_=turned_result[:])
